import numpy as np
import ml_dtypes


def mxq(x, axis, fmt="e4m3"):
    dtype, down = {"e4m3": (ml_dtypes.float8_e4m3fn, 7), "e5m2": (ml_dtypes.float8_e5m2, 14)}[fmt]
    v = np.moveaxis(np.asarray(x, np.float32).astype(ml_dtypes.bfloat16).astype(np.float64), axis, -1)
    blocks = v.reshape(v.shape[:-1] + (-1, 32))
    amax = np.abs(blocks).max(-1, keepdims=True)
    byte = np.maximum(np.where(amax > 0, np.frexp(amax)[1] - 1 + 127, 0) - down, 1)
    scale = np.exp2(byte - 127.0)
    codes = (blocks / scale).astype(np.float32).astype(dtype).astype(np.float64)
    return np.moveaxis((codes * scale).reshape(v.shape), -1, axis)


WIDE = False


def mx_kscale(k):
    if not WIDE:
        return np.ones(k)
    levels = np.array([10, -10, 5, -5, 0])
    if k % 512:
        return np.exp2(np.random.permutation(np.resize(levels, k // 32))).repeat(32)
    a = np.empty((k // 512, 16))
    for p in range(k // 512):
        a[p, :8] = np.random.permutation(np.resize(levels, 8))
        for g in range(8):
            far = levels[np.abs(levels - a[p, g]) >= 10]
            a[p, g + 8] = far[np.random.randint(len(far))]
    return np.exp2(a.ravel()).repeat(32)


BF16 = ml_dtypes.bfloat16


def bf(x):
    return np.asarray(x, np.float32).astype(BF16)


def f64(x):
    return np.asarray(x).astype(np.float64)


B, C, H, W = 128, 1024, 3, 3
C3, P = 3 * C, H * W
EPS = 1e-5


def setup_inputs():
    s = mx_kscale(C3)
    n = np.random.standard_normal
    return {
        "fv": bf(n((B, C3, H, W)) * s[None, :, None, None]),
        "ft": bf(n((B, C))),
        "W1": bf(n((C, C3)) / np.sqrt(C3) / s[None, :]),
        "b1": bf(n(C) * 0.3),
        "g1": bf(1.0 + 0.1 * n(C)),
        "be1": bf(n(C) * 0.3),
        "m1": bf(n(C) * 0.3),
        "v1": bf(np.random.uniform(0.5, 1.5, C)),
        "Wfc1": bf(n((C, C)) * 0.7 / np.sqrt(C)),
        "bfc1": bf(n(C) * 0.3),
    }


def reference(fv, ft, W1, b1, g1, be1, m1, v1, Wfc1, bfc1):
    x = (mxq(f64(W1), 1, "e4m3") @ mxq(f64(fv).reshape(B, C3, P), 1, "e4m3")) + f64(b1)[None, :, None]
    s = f64(g1) / np.sqrt(f64(v1) + EPS)
    fv1 = np.maximum(x * s[None, :, None] + (f64(be1) - f64(m1) * s)[None, :, None], 0.0)
    ft1 = f64(ft) @ f64(Wfc1).T + f64(bfc1)
    out = fv1 + fv1 * ft1[:, :, None]
    return out.reshape(B, C, H, W)

@@ -1,0 +1,363 @@
+from contextlib import ExitStack
+
+import concourse.mybir as mybir
+from concourse.masks import make_identity
+
+F32 = mybir.dt.float32
+BF16 = mybir.dt.bfloat16
+U32 = mybir.dt.uint32
+U8 = mybir.dt.uint8
+FP8X4 = mybir.dt.float8_e4m3fn_x4
+ACT = mybir.ActivationFunctionType
+ALU = mybir.AluOpType
+
+P = 128
+B = 128
+C = 1024
+C3 = 3072
+PIX = 9
+GROUPS = 6
+OT = 8
+COLS = PIX * B
+EPS = 1e-5
+PATH = ("tensor", "tensor", "vector", "tensor", "vector", "tensor", "vector", "tensor")
+FLOPS = 2 * C * C3 * COLS + 2 * B * C * C
+
+
+def tile_joint_module_pa_kernel(tc, fv, ft, W1, b1, g1, be1, m1, v1, Wfc1, bfc1, out):
+    nc = tc.nc
+    with ExitStack() as ctx:
+        const = ctx.enter_context(tc.tile_pool(name="const", bufs=1))
+        keep = ctx.enter_context(tc.tile_pool(name="keep", bufs=1))
+        stage = ctx.enter_context(tc.tile_pool(name="stage", bufs=2))
+        psum = ctx.enter_context(tc.psum_pool(name="psum", bufs=8))
+
+        fv_flat = fv.rearrange("b c h w -> b (c h w)")
+        out_flat = out.rearrange("b o h w -> b (o h w)")
+        wfc_view = Wfc1.rearrange("(t p) k -> p t k", p=P)
+
+        ptile = const.tile([P, P], BF16)
+        nc.vector.memset(ptile[:], 0.0)
+        bt = const.tile([P, C], BF16)
+        nc.vector.memset(bt[:], 0.0)
+        ones = const.tile([P, P], BF16)
+        nc.vector.memset(ones[:], 1.0)
+        for v, vec in enumerate((b1, g1, be1, m1, v1, bfc1)):
+            nc.sync.dma_start(out=ptile[8 * v : 8 * v + 8, :], in_=vec.rearrange("(t p) -> t p", p=P))
+        nc.scalar.dma_start(out=bt[0:1, :], in_=bfc1.rearrange("(a n) -> a n", a=1))
+        ftraw = const.tile([P, C], BF16)
+        nc.sync.dma_start(out=ftraw[:], in_=ft)
+        warm = const.tile([P, 1], F32)
+        nc.vector.memset(warm[:], 1.0)
+        nc.scalar.sqrt(out=warm[:], in_=warm[:])
+        ident_f = const.tile([P, P], F32)
+        make_identity(nc, ident_f[:])
+        ident_b = const.tile([P, P], BF16)
+        make_identity(nc, ident_b[:])
+
+        fvc = keep.tile([P, GROUPS, COLS], U32, align_bytes=64)
+        fvs = keep.tile([P, GROUPS, COLS], U8, align_bytes=64)
+        w1c = keep.tile([P, OT, GROUPS * P], U32, align_bytes=64)
+        w1s = keep.tile([P, OT, GROUPS * P], U8, align_bytes=64)
+        ftT = keep.tile([P, 4 * B], F32)
+        gate = keep.tile([P, C], F32, align_bytes=64)
+        bp1 = keep.tile([P, OT], F32)
+
+        pools = {}
+        fvraw = {}
+        wraw = {}
+        wfraw = {}
+
+        def load_fv(g):
+            raw = pools["front"].tile([P, 512 * PIX], BF16, tag="fvraw", bufs=3, name="fvraw%d" % g)
+            nc.sync.dma_start(out=raw[:], in_=fv_flat[:, g * 4608 : (g + 1) * 4608])
+            fvraw[g] = raw
+
+        def load_w(ot):
+            raw = stage.tile([P, C3], BF16, tag="wraw", bufs=3, name="wraw%d" % ot)
+            nc.sync.dma_start(out=raw[:], in_=W1[ot * P : (ot + 1) * P, :])
+            wraw[ot] = raw
+
+        def load_wf(i):
+            raw = stage.tile([P, 2, C], BF16, tag="wfraw", bufs=2, name="wfraw%d" % i)
+            nc.sync.dma_start(out=raw[:], in_=wfc_view[:, 2 * i : 2 * i + 2, :])
+            wfraw[i] = raw
+
+        tsbs = {}
+
+        def fv_transposes(g):
+            words = fvraw[g][:].bitcast(F32).rearrange("b (p u m) -> b u p m", p=P, u=2, m=PIX)
+            tsb = pools["front"].tile([P, 2560], F32, tag="tsb", bufs=2, name="tsb%d" % g)
+            tw = tsb[:].rearrange("p (m b u) -> p m b u", m=10, b=B, u=2)
+            for m0 in range(0, PIX, 2):
+                nm = min(2, PIX - m0)
+                bank = psum.tile([P, 2, 2, B], F32, tag="bank", name="fvbank")
+                for mm in range(nm):
+                    for u in range(2):
+                        nc.tensor.transpose(bank[:, mm, u, :], words[:, u, :, m0 + mm], ident_f[:])
+                nc.scalar.copy(
+                    out=tw[:, m0 : m0 + nm, :, :],
+                    in_=bank[:, 0:nm, :, :].rearrange("p m u b -> p m b u"),
+                )
+            tsbs[g] = tsb
+
+        def fv_regroup(g):
+            fb = tsbs[g][:].bitcast(BF16)
+            gr = pools["front"].tile([P, PIX * 512], BF16, tag="gr", bufs=2, align_bytes=64, name="gr%d" % g)
+            grv = gr[:].rearrange("p (q j a) -> p q j a", q=PIX, j=256, a=2)
+            even = (
+                fb[:, 0:4098]
+                .rearrange("p (a c) -> p a c", a=2)[:, :, 0:2048]
+                .rearrange("p a (n j h) -> p a n j h", n=4, j=256, h=2)[:, :, :, :, 0]
+                .rearrange("p a n j -> p n j a")
+            )
+            odd = (
+                fb[:, 1:5119]
+                .rearrange("p (a c) -> p a c", a=2)[:, :, 0:2048]
+                .rearrange("p a (n j h) -> p a n j h", n=4, j=256, h=2)[:, :, :, :, 0]
+                .rearrange("p a n j -> p n j a")
+            )
+            last = (
+                fb[:, 512:4610]
+                .rearrange("p (a c) -> p a c", a=2)[:, :, 1536:2048]
+                .rearrange("p a (j h) -> p a j h", j=256, h=2)[:, :, :, 0]
+                .rearrange("p a j -> p j a")
+            )
+            pairs = grv[:, 0:8, :, :].rearrange("p (n two) j a -> p two n j a", two=2)
+            nc.vector.tensor_copy(out=pairs[:, 0, :, :, :], in_=even)
+            nc.vector.tensor_copy(out=pairs[:, 1, :, :, :], in_=odd)
+            nc.vector.tensor_copy(out=grv[:, 8, :, :], in_=last)
+            return gr
+
+        def fv_quant(g, gr):
+            nc.vector.quantize_mx(
+                out=fvc[:, g, 0:1024].bitcast(FP8X4), scales=fvs[:, g, 0:1024], in_=gr[:, 0:4096]
+            )
+            nc.vector.quantize_mx(
+                out=fvc[:, g, 1024:1152].bitcast(FP8X4), scales=fvs[:, g, 1024:1152], in_=gr[:, 4096:4608]
+            )
+
+        def w_tile(ot):
+            words = wraw[ot][:].bitcast(F32)
+            wgr = stage.tile([P, C3], BF16, tag="wgr", bufs=2, align_bytes=64, name="wgr%d" % ot)
+            wv = wgr[:].bitcast(F32).rearrange("p (g o u) -> p g o u", g=GROUPS, o=P, u=2)
+            for g0 in range(0, GROUPS, 2):
+                bank = psum.tile([P, 2, 2, P], F32, tag="bank", name="wbank")
+                for gg in range(2):
+                    for u in range(2):
+                        k0 = 256 * (g0 + gg)
+                        nc.tensor.transpose(bank[:, gg, u, :], words[:, k0 + u : k0 + 256 : 2], ident_f[:])
+                nc.scalar.copy(
+                    out=wv[:, g0 : g0 + 2, :, :], in_=bank[:].rearrange("p g u o -> p g o u")
+                )
+            return wgr
+
+        def w_quant(ot, wgr):
+            nc.vector.quantize_mx(
+                out=w1c[:, ot, 0:512].bitcast(FP8X4), scales=w1s[:, ot, 0:512], in_=wgr[:, 0:2048]
+            )
+            nc.vector.quantize_mx(
+                out=w1c[:, ot, 512:768].bitcast(FP8X4), scales=w1s[:, ot, 512:768], in_=wgr[:, 2048:3072]
+            )
+
+        def params():
+            pbank = psum.tile([P, P], BF16, tag="bank", name="pbank")
+            nc.tensor.transpose(pbank[:], ptile[:], ident_b[:])
+            prm = const.tile([P, 48], F32)
+            nc.vector.tensor_copy(out=prm[:], in_=pbank[:, 0:48])
+            nc.vector.tensor_scalar_add(out=bp1[:], in0=prm[:, 40:48], scalar1=1.0)
+            s_t = const.tile([P, OT], F32)
+            t_t = const.tile([P, OT], F32)
+            tmp = const.tile([P, OT], F32)
+            nc.vector.tensor_scalar_add(out=tmp[:], in0=prm[:, 32:40], scalar1=EPS)
+            nc.scalar.sqrt(out=tmp[:], in_=tmp[:])
+            nc.vector.reciprocal(out=tmp[:], in_=tmp[:])
+            nc.vector.tensor_mul(out=s_t[:], in0=prm[:, 8:16], in1=tmp[:])
+            nc.vector.tensor_sub(out=t_t[:], in0=prm[:, 0:8], in1=prm[:, 24:32])
+            nc.vector.tensor_mul(out=t_t[:], in0=t_t[:], in1=s_t[:])
+            nc.vector.tensor_add(out=t_t[:], in0=t_t[:], in1=prm[:, 16:24])
+            return s_t, t_t
+
+        def ft_transposes():
+            words = ftraw[:].bitcast(F32)
+            bank = psum.tile([P, 4, B], F32, tag="bank", name="ftbank")
+            for kc in range(4):
+                nc.tensor.transpose(bank[:, kc, :], words[:, kc * P : (kc + 1) * P], ident_f[:])
+            nc.scalar.copy(out=ftT[:], in_=bank[:].rearrange("p k b -> p (k b)"))
+
+        wfts = {}
+
+        def gate_transposes(ot):
+            bank = psum.tile([P, 4, P], F32, tag="bank", name="wfbank")
+            words = wfraw[ot // 2][:, ot % 2, :].bitcast(F32)
+            for kc in range(4):
+                nc.tensor.transpose(bank[:, kc, :], words[:, kc * P : (kc + 1) * P], ident_f[:])
+            wft = stage.tile([P, 4 * P], F32, tag="wft", bufs=4, name="wft")
+            nc.scalar.copy(out=wft[:], in_=bank[:].rearrange("p k o -> p (k o)"))
+            wfts[ot] = wft
+
+        def gate_tile(ot):
+            wv = wfts[ot][:].bitcast(BF16).rearrange("p (k o e) -> p k o e", k=4, o=P, e=2)
+            fvw = ftT[:].bitcast(BF16).rearrange("p (k b e) -> p k b e", k=4, b=B, e=2)
+            cols = slice(ot * P, (ot + 1) * P)
+            acc = psum.tile([P, P], F32, tag="bank", name="gbank")
+            on_vector = PATH[ot] == "vector"
+            for kc in range(4):
+                for e in range(2):
+                    nc.tensor.matmul(
+                        acc[:],
+                        lhsT=(wv if on_vector else fvw)[:, kc, :, e],
+                        rhs=(fvw if on_vector else wv)[:, kc, :, e],
+                        start=(kc == 0 and e == 0),
+                        stop=(on_vector and kc == 3 and e == 1),
+                    )
+            if on_vector:
+                gt = stage.tile([P, B], F32, tag="gt", bufs=2, align_bytes=64, name="gt")
+                nc.scalar.activation(out=gt[:], in_=acc[:], func=ACT.Identity, bias=bp1[:, ot : ot + 1], scale=1.0)
+                nc.vector.transpose(out=gate[:, cols], in_=gt[:])
+            else:
+                nc.tensor.matmul(acc[:], lhsT=ones[:], rhs=bt[:, cols], start=False, stop=True)
+                nc.scalar.activation(out=gate[:, cols], in_=acc[:], func=ACT.Copy, bias=1.0, scale=1.0)
+
+        CHUNKS = ((0, 512), (512, 512), (1024, 128))
+
+        def mx_pass(acc, ot, g, c0, n):
+            nc.tensor.matmul_mx(
+                out=acc[:],
+                lhsT=w1c[:, ot, g * P : (g + 1) * P].bitcast(FP8X4),
+                lhsT_scale=w1s[:, ot, g * P : (g + 1) * P],
+                rhs=fvc[:, g, c0 : c0 + n].bitcast(FP8X4),
+                rhs_scale=fvs[:, g, c0 : c0 + n],
+                start=(g == 0),
+                stop=(g == GROUPS - 1),
+            )
+
+        def bn_relu(y, acc, ot, c0, n, s_t, t_t):
+            nc.scalar.activation(
+                out=y[:, c0 : c0 + n],
+                in_=acc[:],
+                func=ACT.Relu,
+                bias=t_t[:, ot : ot + 1],
+                scale=s_t[:, ot : ot + 1],
+            )
+
+        def conv(ot, s_t, t_t, chunks, y):
+            for c0, n in chunks:
+                acc = psum.tile([P, n], F32, tag="bank", name="acc")
+                for g in range(GROUPS):
+                    mx_pass(acc, ot, g, c0, n)
+                bn_relu(y, acc, ot, c0, n, s_t, t_t)
+
+        def new_y(ot):
+            y = pools["back"].tile([P, COLS], F32, tag="y", bufs=3, align_bytes=64, name="y%d" % ot)
+            return y
+
+        def finish_on_vector(ot, y):
+            yt = pools["back"].tile([P, COLS], F32, tag="yt", bufs=2, align_bytes=64, name="yt%d" % ot)
+            nc.vector.transpose(out=yt[:, 0:1024], in_=y[:, 0:1024])
+            nc.vector.transpose(out=yt[:, 1024:1152], in_=y[:, 1024:1152])
+            osb = pools["back"].tile([P, P, PIX], F32, tag="osb", bufs=4, name="osbv%d" % ot)
+            nc.vector.tensor_tensor(
+                out=osb[:],
+                in0=yt[:].rearrange("p (x c) -> p c x", x=PIX),
+                in1=gate[:, ot * P : (ot + 1) * P].unsqueeze(2).to_broadcast([P, P, PIX]),
+                op=ALU.mult,
+            )
+            rows = out_flat.rearrange("(j l) f -> l j f", l=32)
+            for i in range(4):
+                f0 = (ot * P + 32 * i) * PIX
+                nc.sync.dma_start(
+                    out=rows[:, :, f0 : f0 + 32 * PIX],
+                    in_=osb[32 * i : 32 * i + 32, :, :].rearrange("l (j o) x -> l j (o x)", j=4),
+                )
+
+        def finish(ot, y):
+            if PATH[ot] == "vector":
+                finish_on_vector(ot, y)
+                return
+            planes = pools["back"].tile([P, PIX, P], F32, tag="planes", bufs=3, name="planes%d" % ot)
+            for x0 in range(0, PIX, 4):
+                nx = min(4, PIX - x0)
+                z = psum.tile([P, nx, P], F32, tag="bank", name="z")
+                for i in range(nx):
+                    q = x0 + i
+                    nc.tensor.transpose(z[:, i, :], y[:, q * B : (q + 1) * B], ident_f[:])
+                nc.scalar.copy(out=planes[:, x0 : x0 + nx, :], in_=z[:])
+            step = 64 if ot == OT - 1 else P
+            for i0 in range(0, P, step):
+                osb = pools["back"].tile([P, step, PIX], F32, tag="osb", bufs=4, name="osb%d" % ot)
+                o0 = ot * P + i0
+                nc.vector.tensor_tensor(
+                    out=osb[:],
+                    in0=planes[:, :, i0 : i0 + step].rearrange("b x o -> b o x"),
+                    in1=gate[:, o0 : o0 + step].unsqueeze(2).to_broadcast([P, step, PIX]),
+                    op=ALU.mult,
+                )
+                nc.sync.dma_start(
+                    out=out_flat[:, o0 * PIX : (o0 + step) * PIX], in_=osb[:].rearrange("b o x -> b (o x)")
+                )
+
+        EARLY = ((0, 0), (0, 512), (1, 0), (1, 512))
+        with tc.tile_pool(name="front", bufs=2) as front:
+            pools["front"] = front
+            load_w(0)
+            load_fv(0)
+            load_w(1)
+            load_fv(1)
+            load_fv(2)
+            s_t, t_t = params()
+            ft_transposes()
+            wgrs = {0: w_tile(0)}
+            fv_transposes(0)
+            w_quant(0, wgrs[0])
+            wgrs[1] = w_tile(1)
+            fv_transposes(1)
+            grs = {0: fv_regroup(0)}
+            open_acc = {}
+            extra = {0: lambda: load_w(2), 1: lambda: load_wf(0), 2: lambda: load_wf(1)}
+            for g in range(GROUPS):
+                if g + 3 < GROUPS:
+                    load_fv(g + 3)
+                    extra[g]()
+                if g + 2 < GROUPS:
+                    fv_transposes(g + 2)
+                if g + 1 < GROUPS:
+                    grs[g + 1] = fv_regroup(g + 1)
+                fv_quant(g, grs[g])
+                if g == 0:
+                    w_quant(1, wgrs[1])
+                for ot, c0 in EARLY:
+                    if g == 0:
+                        acc = psum.tile([P, 512], F32, tag="bank", name="early")
+                        open_acc[(ot, c0)] = acc
+                    mx_pass(open_acc[(ot, c0)], ot, g, c0, 512)
+                if g == 3:
+                    for ot in range(4):
+                        gate_transposes(ot)
+                    load_wf(2)
+                    load_wf(3)
+                    for ot in range(4):
+                        gate_tile(ot)
+                if g == 5:
+                    for ot in range(4, OT):
+                        gate_transposes(ot)
+                    for ot in range(4, OT):
+                        gate_tile(ot)
+        pools["back"] = ctx.enter_context(tc.tile_pool(name="back", bufs=2))
+        ys = {}
+        for ot in range(OT):
+            ys[ot] = new_y(ot)
+            if ot < 2:
+                bn_relu(ys[ot], open_acc[(ot, 0)], ot, 0, 512, s_t, t_t)
+                bn_relu(ys[ot], open_acc[(ot, 512)], ot, 512, 512, s_t, t_t)
+                conv(ot, s_t, t_t, CHUNKS[2:], ys[ot])
+            else:
+                conv(ot, s_t, t_t, CHUNKS, ys[ot])
+            if ot + 3 < OT:
+                load_w(ot + 3)
+            if ot + 2 < OT:
+                wgr = w_tile(ot + 2)
+                w_quant(ot + 2, wgr)
+            if ot >= 1:
+                finish(ot - 1, ys[ot - 1])
+        finish(OT - 1, ys[OT - 1])

@@ -258,9 +258,12 @@ def tile_joint_module_pa_kernel(tc, fv, ft, W1, b1, g1, be1, m1, v1, Wfc1, bfc1,
             nc.vector.transpose(out=yt[:, 1024:1152], in_=y[:, 1024:1152])
             osb = pools["back"].tile([P, P, PIX], F32, tag="osb", bufs=4, name="osbv%d" % ot)
             nc.vector.tensor_tensor(
-                out=osb[:],
-                in0=yt[:].rearrange("p (x c) -> p c x", x=PIX),
-                in1=gate[:, ot * P : (ot + 1) * P].unsqueeze(2).to_broadcast([P, P, PIX]),
+                out=osb[:].rearrange("p (n i) x -> p n x i", i=4),
+                in0=yt[:].rearrange("p (x n i) -> p n x i", x=PIX, i=4),
+                in1=gate[:, ot * P : (ot + 1) * P]
+                .rearrange("p (n i) -> p n i", i=4)
+                .unsqueeze(2)
+                .to_broadcast([P, P // 4, PIX, 4]),
                 op=ALU.mult,
             )
             rows = out_flat.rearrange("(j l) f -> l j f", l=32)
@@ -288,9 +291,12 @@ def tile_joint_module_pa_kernel(tc, fv, ft, W1, b1, g1, be1, m1, v1, Wfc1, bfc1,
                 osb = pools["back"].tile([P, step, PIX], F32, tag="osb", bufs=4, name="osb%d" % ot)
                 o0 = ot * P + i0
                 nc.vector.tensor_tensor(
-                    out=osb[:],
-                    in0=planes[:, :, i0 : i0 + step].rearrange("b x o -> b o x"),
-                    in1=gate[:, o0 : o0 + step].unsqueeze(2).to_broadcast([P, step, PIX]),
+                    out=osb[:].rearrange("b (n i) x -> b n x i", i=4),
+                    in0=planes[:, :, i0 : i0 + step].rearrange("b x (n i) -> b n x i", i=4),
+                    in1=gate[:, o0 : o0 + step]
+                    .rearrange("b (n i) -> b n i", i=4)
+                    .unsqueeze(2)
+                    .to_broadcast([P, step // 4, PIX, 4]),
                     op=ALU.mult,
                 )
                 nc.sync.dma_start(

@@ -20,6 +20,7 @@ GROUPS = 6
 OT = 8
 COLS = PIX * B
 EPS = 1e-5
+FV_PARTS = (2, 1, 1, 1, 1, 1)
 PATH = ("tensor", "tensor", "vector", "tensor", "vector", "tensor", "vector", "tensor")
 FLOPS = 2 * C * C3 * COLS + 2 * B * C * C
 
@@ -37,23 +38,25 @@ def tile_joint_module_pa_kernel(tc, fv, ft, W1, b1, g1, be1, m1, v1, Wfc1, bfc1,
         wfc_view = Wfc1.rearrange("(t p) k -> p t k", p=P)
 
         ptile = const.tile([P, P], BF16)
-        nc.vector.memset(ptile[:], 0.0)
         bt = const.tile([P, C], BF16)
-        nc.vector.memset(bt[:], 0.0)
         ones = const.tile([P, P], BF16)
-        nc.vector.memset(ones[:], 1.0)
-        for v, vec in enumerate((b1, g1, be1, m1, v1, bfc1)):
-            nc.sync.dma_start(out=ptile[8 * v : 8 * v + 8, :], in_=vec.rearrange("(t p) -> t p", p=P))
-        nc.scalar.dma_start(out=bt[0:1, :], in_=bfc1.rearrange("(a n) -> a n", a=1))
         ftraw = const.tile([P, C], BF16)
-        nc.sync.dma_start(out=ftraw[:], in_=ft)
         warm = const.tile([P, 1], F32)
         nc.vector.memset(warm[:], 1.0)
         nc.scalar.sqrt(out=warm[:], in_=warm[:])
         ident_f = const.tile([P, P], F32)
         make_identity(nc, ident_f[:])
+        nc.gpsimd.memset(ptile[:], 0.0)
         ident_b = const.tile([P, P], BF16)
         make_identity(nc, ident_b[:])
+        nc.gpsimd.memset(bt[:], 0.0)
+        nc.gpsimd.memset(ones[:], 1.0)
+
+        def load_small():
+            for v, vec in enumerate((b1, g1, be1, m1, v1, bfc1)):
+                nc.sync.dma_start(out=ptile[8 * v : 8 * v + 8, :], in_=vec.rearrange("(t p) -> t p", p=P))
+            nc.sync.dma_start(out=bt[0:1, :], in_=bfc1.rearrange("(a n) -> a n", a=1))
+            nc.sync.dma_start(out=ftraw[:], in_=ft)
 
         fvc = keep.tile([P, GROUPS, COLS], U32, align_bytes=64)
         fvs = keep.tile([P, GROUPS, COLS], U8, align_bytes=64)
@@ -70,63 +73,52 @@ def tile_joint_module_pa_kernel(tc, fv, ft, W1, b1, g1, be1, m1, v1, Wfc1, bfc1,
 
         def load_fv(g):
             raw = pools["front"].tile([P, 512 * PIX], BF16, tag="fvraw", bufs=3, name="fvraw%d" % g)
-            nc.sync.dma_start(out=raw[:], in_=fv_flat[:, g * 4608 : (g + 1) * 4608])
+            part = 4608 // FV_PARTS[g]
+            for c in range(0, 4608, part):
+                nc.sync.dma_start(
+                    out=raw[:, c : c + part], in_=fv_flat[:, g * 4608 + c : g * 4608 + c + part]
+                )
             fvraw[g] = raw
 
         def load_w(ot):
-            raw = stage.tile([P, C3], BF16, tag="wraw", bufs=3, name="wraw%d" % ot)
+            raw = stage.tile([P, C3], BF16, tag="wraw", bufs=4, name="wraw%d" % ot)
             nc.sync.dma_start(out=raw[:], in_=W1[ot * P : (ot + 1) * P, :])
             wraw[ot] = raw
 
         def load_wf(i):
-            raw = stage.tile([P, 2, C], BF16, tag="wfraw", bufs=2, name="wfraw%d" % i)
+            raw = stage.tile([P, 2, C], BF16, tag="wfraw", bufs=4, name="wfraw%d" % i)
             nc.sync.dma_start(out=raw[:], in_=wfc_view[:, 2 * i : 2 * i + 2, :])
             wfraw[i] = raw
 
-        tsbs = {}
-
-        def fv_transposes(g):
-            words = fvraw[g][:].bitcast(F32).rearrange("b (p u m) -> b u p m", p=P, u=2, m=PIX)
-            tsb = pools["front"].tile([P, 2560], F32, tag="tsb", bufs=2, name="tsb%d" % g)
-            tw = tsb[:].rearrange("p (m b u) -> p m b u", m=10, b=B, u=2)
-            for m0 in range(0, PIX, 2):
-                nm = min(2, PIX - m0)
-                bank = psum.tile([P, 2, 2, B], F32, tag="bank", name="fvbank")
-                for mm in range(nm):
-                    for u in range(2):
-                        nc.tensor.transpose(bank[:, mm, u, :], words[:, u, :, m0 + mm], ident_f[:])
-                nc.scalar.copy(
-                    out=tw[:, m0 : m0 + nm, :, :],
-                    in_=bank[:, 0:nm, :, :].rearrange("p m u b -> p m b u"),
-                )
-            tsbs[g] = tsb
+        pres = {}
 
         def fv_regroup(g):
-            fb = tsbs[g][:].bitcast(BF16)
+            src = fvraw[g][:].rearrange("b (p u e x) -> b u p e x", p=P, u=2, e=2, x=PIX)
+            pre = pools["front"].tile([P, PIX * 512], BF16, tag="pre", bufs=2, name="pre%d" % g)
+            dst = pre[:].rearrange("b (x u p e) -> b u p e x", x=PIX, u=2, p=P, e=2)
+            part = P // FV_PARTS[g]
+            for p0 in range(0, P, part):
+                for x0 in range(0, PIX, 3):
+                    nc.vector.tensor_copy(
+                        out=dst[:, :, p0 : p0 + part, :, x0 : x0 + 3],
+                        in_=src[:, :, p0 : p0 + part, :, x0 : x0 + 3],
+                    )
+            pres[g] = pre
+
+        def fv_transposes(g):
+            words = pres[g][:].bitcast(F32).rearrange("b (x u p) -> b x u p", x=PIX, u=2, p=P)
             gr = pools["front"].tile([P, PIX * 512], BF16, tag="gr", bufs=2, align_bytes=64, name="gr%d" % g)
-            grv = gr[:].rearrange("p (q j a) -> p q j a", q=PIX, j=256, a=2)
-            even = (
-                fb[:, 0:4098]
-                .rearrange("p (a c) -> p a c", a=2)[:, :, 0:2048]
-                .rearrange("p a (n j h) -> p a n j h", n=4, j=256, h=2)[:, :, :, :, 0]
-                .rearrange("p a n j -> p n j a")
-            )
-            odd = (
-                fb[:, 1:5119]
-                .rearrange("p (a c) -> p a c", a=2)[:, :, 0:2048]
-                .rearrange("p a (n j h) -> p a n j h", n=4, j=256, h=2)[:, :, :, :, 0]
-                .rearrange("p a n j -> p n j a")
-            )
-            last = (
-                fb[:, 512:4610]
-                .rearrange("p (a c) -> p a c", a=2)[:, :, 1536:2048]
-                .rearrange("p a (j h) -> p a j h", j=256, h=2)[:, :, :, 0]
-                .rearrange("p a j -> p j a")
-            )
-            pairs = grv[:, 0:8, :, :].rearrange("p (n two) j a -> p two n j a", two=2)
-            nc.vector.tensor_copy(out=pairs[:, 0, :, :, :], in_=even)
-            nc.vector.tensor_copy(out=pairs[:, 1, :, :, :], in_=odd)
-            nc.vector.tensor_copy(out=grv[:, 8, :, :], in_=last)
+            grw = gr[:].bitcast(F32).rearrange("p (x b u) -> p x b u", x=PIX, b=B, u=2)
+            for x0 in range(0, PIX, 2):
+                nx = min(2, PIX - x0)
+                bank = psum.tile([P, 2, 2, B], F32, tag="bank", name="fvbank")
+                for x in range(nx):
+                    for u in range(2):
+                        nc.tensor.transpose(bank[:, x, u, :], words[:, x0 + x, u, :], ident_f[:])
+                nc.scalar.copy(
+                    out=grw[:, x0 : x0 + nx, :, :],
+                    in_=bank[:, 0:nx, :, :].rearrange("p x u b -> p x b u"),
+                )
             return gr
 
         def fv_quant(g, gr):
@@ -139,7 +131,7 @@ def tile_joint_module_pa_kernel(tc, fv, ft, W1, b1, g1, be1, m1, v1, Wfc1, bfc1,
 
         def w_tile(ot):
             words = wraw[ot][:].bitcast(F32)
-            wgr = stage.tile([P, C3], BF16, tag="wgr", bufs=2, align_bytes=64, name="wgr%d" % ot)
+            wgr = stage.tile([P, C3], BF16, tag="wgr", bufs=3, align_bytes=64, name="wgr%d" % ot)
             wv = wgr[:].bitcast(F32).rearrange("p (g o u) -> p g o u", g=GROUPS, o=P, u=2)
             for g0 in range(0, GROUPS, 2):
                 bank = psum.tile([P, 2, 2, P], F32, tag="bank", name="wbank")
@@ -306,49 +298,47 @@ def tile_joint_module_pa_kernel(tc, fv, ft, W1, b1, g1, be1, m1, v1, Wfc1, bfc1,
         EARLY = ((0, 0), (0, 512), (1, 0), (1, 512))
         with tc.tile_pool(name="front", bufs=2) as front:
             pools["front"] = front
-            load_w(0)
             load_fv(0)
-            load_w(1)
+            load_w(0)
+            load_small()
             load_fv(1)
+            load_w(1)
             load_fv(2)
-            s_t, t_t = params()
-            ft_transposes()
+            load_w(2)
+            fv_regroup(0)
             wgrs = {0: w_tile(0)}
-            fv_transposes(0)
+            fv_regroup(1)
+            grs = {0: fv_transposes(0)}
             w_quant(0, wgrs[0])
             wgrs[1] = w_tile(1)
-            fv_transposes(1)
-            grs = {0: fv_regroup(0)}
+            s_t, t_t = params()
+            ft_transposes()
             open_acc = {}
-            extra = {0: lambda: load_w(2), 1: lambda: load_wf(0), 2: lambda: load_wf(1)}
             for g in range(GROUPS):
                 if g + 3 < GROUPS:
                     load_fv(g + 3)
-                    extra[g]()
+                if g + 3 < OT:
+                    load_w(g + 3)
+                if g >= 2:
+                    load_wf(g - 2)
                 if g + 2 < GROUPS:
-                    fv_transposes(g + 2)
+                    fv_regroup(g + 2)
                 if g + 1 < GROUPS:
-                    grs[g + 1] = fv_regroup(g + 1)
+                    grs[g + 1] = fv_transposes(g + 1)
                 fv_quant(g, grs[g])
-                if g == 0:
-                    w_quant(1, wgrs[1])
+                w_quant(g + 1, wgrs[g + 1])
                 for ot, c0 in EARLY:
                     if g == 0:
                         acc = psum.tile([P, 512], F32, tag="bank", name="early")
                         open_acc[(ot, c0)] = acc
                     mx_pass(open_acc[(ot, c0)], ot, g, c0, 512)
-                if g == 3:
-                    for ot in range(4):
-                        gate_transposes(ot)
-                    load_wf(2)
-                    load_wf(3)
-                    for ot in range(4):
-                        gate_tile(ot)
-                if g == 5:
-                    for ot in range(4, OT):
-                        gate_transposes(ot)
-                    for ot in range(4, OT):
-                        gate_tile(ot)
+                wgrs[g + 2] = w_tile(g + 2)
+            w_quant(OT - 1, wgrs[OT - 1])
+            for half in (range(0, 4), range(4, OT)):
+                for ot in half:
+                    gate_transposes(ot)
+                for ot in half:
+                    gate_tile(ot)
         pools["back"] = ctx.enter_context(tc.tile_pool(name="back", bufs=2))
         ys = {}
         for ot in range(OT):
@@ -359,11 +349,6 @@ def tile_joint_module_pa_kernel(tc, fv, ft, W1, b1, g1, be1, m1, v1, Wfc1, bfc1,
                 conv(ot, s_t, t_t, CHUNKS[2:], ys[ot])
             else:
                 conv(ot, s_t, t_t, CHUNKS, ys[ot])
-            if ot + 3 < OT:
-                load_w(ot + 3)
-            if ot + 2 < OT:
-                wgr = w_tile(ot + 2)
-                w_quant(ot + 2, wgr)
             if ot >= 1:
                 finish(ot - 1, ys[ot - 1])
         finish(OT - 1, ys[OT - 1])

@@ -10,6 +10,7 @@ U8 = mybir.dt.uint8
 FP8X4 = mybir.dt.float8_e4m3fn_x4
 ACT = mybir.ActivationFunctionType
 ALU = mybir.AluOpType
+ENG = mybir.EngineType
 
 P = 128
 B = 128
@@ -21,7 +22,6 @@ OT = 8
 COLS = PIX * B
 EPS = 1e-5
 FV_PARTS = (2, 1, 1, 1, 1, 1)
-PATH = ("tensor", "tensor", "vector", "tensor", "vector", "tensor", "vector", "tensor")
 FLOPS = 2 * C * C3 * COLS + 2 * B * C * C
 
 
@@ -34,12 +34,10 @@ def tile_joint_module_pa_kernel(tc, fv, ft, W1, b1, g1, be1, m1, v1, Wfc1, bfc1,
         psum = ctx.enter_context(tc.psum_pool(name="psum", bufs=8))
 
         fv_flat = fv.rearrange("b c h w -> b (c h w)")
-        out_flat = out.rearrange("b o h w -> b (o h w)")
+        out_rows = out.rearrange("b o h w -> b (o h w)").rearrange("(j l) f -> l j f", l=32)
         wfc_view = Wfc1.rearrange("(t p) k -> p t k", p=P)
 
         ptile = const.tile([P, P], BF16)
-        bt = const.tile([P, C], BF16)
-        ones = const.tile([P, P], BF16)
         ftraw = const.tile([P, C], BF16)
         warm = const.tile([P, 1], F32)
         nc.vector.memset(warm[:], 1.0)
@@ -49,13 +47,10 @@ def tile_joint_module_pa_kernel(tc, fv, ft, W1, b1, g1, be1, m1, v1, Wfc1, bfc1,
         nc.gpsimd.memset(ptile[:], 0.0)
         ident_b = const.tile([P, P], BF16)
         make_identity(nc, ident_b[:])
-        nc.gpsimd.memset(bt[:], 0.0)
-        nc.gpsimd.memset(ones[:], 1.0)
 
         def load_small():
             for v, vec in enumerate((b1, g1, be1, m1, v1, bfc1)):
                 nc.sync.dma_start(out=ptile[8 * v : 8 * v + 8, :], in_=vec.rearrange("(t p) -> t p", p=P))
-            nc.sync.dma_start(out=bt[0:1, :], in_=bfc1.rearrange("(a n) -> a n", a=1))
             nc.sync.dma_start(out=ftraw[:], in_=ft)
 
         fvc = keep.tile([P, GROUPS, COLS], U32, align_bytes=64)
@@ -91,6 +86,7 @@ def tile_joint_module_pa_kernel(tc, fv, ft, W1, b1, g1, be1, m1, v1, Wfc1, bfc1,
             wfraw[i] = raw
 
         pres = {}
+        grs = {}
 
         def fv_regroup(g):
             src = fvraw[g][:].rearrange("b (p u e x) -> b u p e x", p=P, u=2, e=2, x=PIX)
@@ -105,12 +101,14 @@ def tile_joint_module_pa_kernel(tc, fv, ft, W1, b1, g1, be1, m1, v1, Wfc1, bfc1,
                     )
             pres[g] = pre
 
-        def fv_transposes(g):
+        def fv_transposes(g, x_from, x_to):
             words = pres[g][:].bitcast(F32).rearrange("b (x u p) -> b x u p", x=PIX, u=2, p=P)
-            gr = pools["front"].tile([P, PIX * 512], BF16, tag="gr", bufs=2, align_bytes=64, name="gr%d" % g)
-            grw = gr[:].bitcast(F32).rearrange("p (x b u) -> p x b u", x=PIX, b=B, u=2)
-            for x0 in range(0, PIX, 2):
-                nx = min(2, PIX - x0)
+            if g not in grs:
+                gr = pools["front"].tile([P, PIX * 512], BF16, tag="gr", bufs=2, align_bytes=64, name="gr%d" % g)
+                grs[g] = gr
+            grw = grs[g][:].bitcast(F32).rearrange("p (x b u) -> p x b u", x=PIX, b=B, u=2)
+            for x0 in range(x_from, x_to, 2):
+                nx = min(2, x_to - x0)
                 bank = psum.tile([P, 2, 2, B], F32, tag="bank", name="fvbank")
                 for x in range(nx):
                     for u in range(2):
@@ -119,9 +117,9 @@ def tile_joint_module_pa_kernel(tc, fv, ft, W1, b1, g1, be1, m1, v1, Wfc1, bfc1,
                     out=grw[:, x0 : x0 + nx, :, :],
                     in_=bank[:, 0:nx, :, :].rearrange("p x u b -> p x b u"),
                 )
-            return gr
 
-        def fv_quant(g, gr):
+        def fv_quant(g):
+            gr = grs[g]
             nc.vector.quantize_mx(
                 out=fvc[:, g, 0:1024].bitcast(FP8X4), scales=fvs[:, g, 0:1024], in_=gr[:, 0:4096]
             )
@@ -129,9 +127,11 @@ def tile_joint_module_pa_kernel(tc, fv, ft, W1, b1, g1, be1, m1, v1, Wfc1, bfc1,
                 out=fvc[:, g, 1024:1152].bitcast(FP8X4), scales=fvs[:, g, 1024:1152], in_=gr[:, 4096:4608]
             )
 
+        wgrs = {}
+
         def w_tile(ot):
             words = wraw[ot][:].bitcast(F32)
-            wgr = stage.tile([P, C3], BF16, tag="wgr", bufs=3, align_bytes=64, name="wgr%d" % ot)
+            wgr = stage.tile([P, C3], BF16, tag="wgr", bufs=2, align_bytes=64, name="wgr%d" % ot)
             wv = wgr[:].bitcast(F32).rearrange("p (g o u) -> p g o u", g=GROUPS, o=P, u=2)
             for g0 in range(0, GROUPS, 2):
                 bank = psum.tile([P, 2, 2, P], F32, tag="bank", name="wbank")
@@ -142,9 +142,10 @@ def tile_joint_module_pa_kernel(tc, fv, ft, W1, b1, g1, be1, m1, v1, Wfc1, bfc1,
                 nc.scalar.copy(
                     out=wv[:, g0 : g0 + 2, :, :], in_=bank[:].rearrange("p g u o -> p g o u")
                 )
-            return wgr
+            wgrs[ot] = wgr
 
-        def w_quant(ot, wgr):
+        def w_quant(ot):
+            wgr = wgrs[ot]
             nc.vector.quantize_mx(
                 out=w1c[:, ot, 0:512].bitcast(FP8X4), scales=w1s[:, ot, 0:512], in_=wgr[:, 0:2048]
             )
@@ -191,25 +192,19 @@ def tile_joint_module_pa_kernel(tc, fv, ft, W1, b1, g1, be1, m1, v1, Wfc1, bfc1,
         def gate_tile(ot):
             wv = wfts[ot][:].bitcast(BF16).rearrange("p (k o e) -> p k o e", k=4, o=P, e=2)
             fvw = ftT[:].bitcast(BF16).rearrange("p (k b e) -> p k b e", k=4, b=B, e=2)
-            cols = slice(ot * P, (ot + 1) * P)
             acc = psum.tile([P, P], F32, tag="bank", name="gbank")
-            on_vector = PATH[ot] == "vector"
             for kc in range(4):
                 for e in range(2):
                     nc.tensor.matmul(
                         acc[:],
-                        lhsT=(wv if on_vector else fvw)[:, kc, :, e],
-                        rhs=(fvw if on_vector else wv)[:, kc, :, e],
+                        lhsT=wv[:, kc, :, e],
+                        rhs=fvw[:, kc, :, e],
                         start=(kc == 0 and e == 0),
-                        stop=(on_vector and kc == 3 and e == 1),
+                        stop=(kc == 3 and e == 1),
                     )
-            if on_vector:
-                gt = stage.tile([P, B], F32, tag="gt", bufs=2, align_bytes=64, name="gt")
-                nc.scalar.activation(out=gt[:], in_=acc[:], func=ACT.Identity, bias=bp1[:, ot : ot + 1], scale=1.0)
-                nc.vector.transpose(out=gate[:, cols], in_=gt[:])
-            else:
-                nc.tensor.matmul(acc[:], lhsT=ones[:], rhs=bt[:, cols], start=False, stop=True)
-                nc.scalar.activation(out=gate[:, cols], in_=acc[:], func=ACT.Copy, bias=1.0, scale=1.0)
+            gt = stage.tile([P, B], F32, tag="gt", bufs=2, align_bytes=64, name="gt")
+            nc.scalar.activation(out=gt[:], in_=acc[:], func=ACT.Identity, bias=bp1[:, ot : ot + 1], scale=1.0)
+            nc.vector.transpose(out=gate[:, ot * P : (ot + 1) * P], in_=gt[:])
 
         CHUNKS = ((0, 512), (512, 512), (1024, 128))
 
@@ -244,58 +239,32 @@ def tile_joint_module_pa_kernel(tc, fv, ft, W1, b1, g1, be1, m1, v1, Wfc1, bfc1,
             y = pools["back"].tile([P, COLS], F32, tag="y", bufs=3, align_bytes=64, name="y%d" % ot)
             return y
 
-        def finish_on_vector(ot, y):
-            yt = pools["back"].tile([P, COLS], F32, tag="yt", bufs=2, align_bytes=64, name="yt%d" % ot)
-            nc.vector.transpose(out=yt[:, 0:1024], in_=y[:, 0:1024])
-            nc.vector.transpose(out=yt[:, 1024:1152], in_=y[:, 1024:1152])
-            osb = pools["back"].tile([P, P, PIX], F32, tag="osb", bufs=4, name="osbv%d" % ot)
-            nc.vector.tensor_tensor(
-                out=osb[:].rearrange("p (n i) x -> p n x i", i=4),
-                in0=yt[:].rearrange("p (x n i) -> p n x i", x=PIX, i=4),
-                in1=gate[:, ot * P : (ot + 1) * P]
-                .rearrange("p (n i) -> p n i", i=4)
-                .unsqueeze(2)
-                .to_broadcast([P, P // 4, PIX, 4]),
-                op=ALU.mult,
-            )
-            rows = out_flat.rearrange("(j l) f -> l j f", l=32)
-            for i in range(4):
-                f0 = (ot * P + 32 * i) * PIX
-                nc.sync.dma_start(
-                    out=rows[:, :, f0 : f0 + 32 * PIX],
-                    in_=osb[32 * i : 32 * i + 32, :, :].rearrange("l (j o) x -> l j (o x)", j=4),
-                )
-
         def finish(ot, y):
-            if PATH[ot] == "vector":
-                finish_on_vector(ot, y)
-                return
-            planes = pools["back"].tile([P, PIX, P], F32, tag="planes", bufs=3, name="planes%d" % ot)
-            for x0 in range(0, PIX, 4):
-                nx = min(4, PIX - x0)
-                z = psum.tile([P, nx, P], F32, tag="bank", name="z")
-                for i in range(nx):
-                    q = x0 + i
-                    nc.tensor.transpose(z[:, i, :], y[:, q * B : (q + 1) * B], ident_f[:])
-                nc.scalar.copy(out=planes[:, x0 : x0 + nx, :], in_=z[:])
-            step = 64 if ot == OT - 1 else P
-            for i0 in range(0, P, step):
-                osb = pools["back"].tile([P, step, PIX], F32, tag="osb", bufs=4, name="osb%d" % ot)
-                o0 = ot * P + i0
+            last = ot == OT - 1
+            yt = pools["back"].tile([P, COLS], F32, tag="yt", bufs=2, align_bytes=64, name="yt%d" % ot)
+            for c0, n in CHUNKS if last else ((0, 1024), (1024, 128)):
+                nc.vector.transpose(out=yt[:, c0 : c0 + n], in_=y[:, c0 : c0 + n])
+            step = 2 if last else 4
+            for j0 in range(0, 4, step):
+                osb = pools["back"].tile([P, 32 * step, PIX], F32, tag="osb", bufs=4, name="osb%d" % ot)
+                nn = 8 * step
                 nc.vector.tensor_tensor(
-                    out=osb[:].rearrange("b (n i) x -> b n x i", i=4),
-                    in0=planes[:, :, i0 : i0 + step].rearrange("b x (n i) -> b n x i", i=4),
-                    in1=gate[:, o0 : o0 + step]
-                    .rearrange("b (n i) -> b n i", i=4)
+                    out=osb[:].rearrange("p (n i) x -> p n x i", i=4),
+                    in0=yt[:].rearrange("p (x n i) -> p n x i", x=PIX, i=4)[:, 8 * j0 : 8 * j0 + nn, :, :],
+                    in1=gate[:, ot * P + 32 * j0 : ot * P + 32 * (j0 + step)]
+                    .rearrange("p (n i) -> p n i", i=4)
                     .unsqueeze(2)
-                    .to_broadcast([P, step // 4, PIX, 4]),
+                    .to_broadcast([P, nn, PIX, 4]),
                     op=ALU.mult,
                 )
-                nc.sync.dma_start(
-                    out=out_flat[:, o0 * PIX : (o0 + step) * PIX], in_=osb[:].rearrange("b o x -> b (o x)")
-                )
+                for i in range(4):
+                    f0 = (ot * P + 32 * i) * PIX
+                    nc.sync.dma_start(
+                        out=out_rows[:, j0 : j0 + step, f0 : f0 + 32 * PIX],
+                        in_=osb[32 * i : 32 * i + 32, :, :].rearrange("l (j o) x -> l j (o x)", j=step),
+                    )
 
-        EARLY = ((0, 0), (0, 512), (1, 0), (1, 512))
+        EARLY = (0, 1)
         with tc.tile_pool(name="front", bufs=2) as front:
             pools["front"] = front
             load_fv(0)
@@ -304,51 +273,63 @@ def tile_joint_module_pa_kernel(tc, fv, ft, W1, b1, g1, be1, m1, v1, Wfc1, bfc1,
             load_fv(1)
             load_w(1)
             load_fv(2)
-            load_w(2)
+            load_wf(0)
             fv_regroup(0)
-            wgrs = {0: w_tile(0)}
+            w_tile(0)
             fv_regroup(1)
-            grs = {0: fv_transposes(0)}
-            w_quant(0, wgrs[0])
-            wgrs[1] = w_tile(1)
+            fv_transposes(0, 0, PIX)
+            w_quant(0)
+            w_tile(1)
             s_t, t_t = params()
             ft_transposes()
+            w_quant(1)
             open_acc = {}
-            for g in range(GROUPS):
-                if g + 3 < GROUPS:
-                    load_fv(g + 3)
-                if g + 3 < OT:
-                    load_w(g + 3)
-                if g >= 2:
-                    load_wf(g - 2)
-                if g + 2 < GROUPS:
-                    fv_regroup(g + 2)
-                if g + 1 < GROUPS:
-                    grs[g + 1] = fv_transposes(g + 1)
-                fv_quant(g, grs[g])
-                w_quant(g + 1, wgrs[g + 1])
-                for ot, c0 in EARLY:
-                    if g == 0:
-                        acc = psum.tile([P, 512], F32, tag="bank", name="early")
-                        open_acc[(ot, c0)] = acc
-                    mx_pass(open_acc[(ot, c0)], ot, g, c0, 512)
-                wgrs[g + 2] = w_tile(g + 2)
-            w_quant(OT - 1, wgrs[OT - 1])
-            for half in (range(0, 4), range(4, OT)):
-                for ot in half:
-                    gate_transposes(ot)
-                for ot in half:
-                    gate_tile(ot)
+            with tc.manual_schedule(engines={ENG.PE}):
+                for g in range(GROUPS):
+                    if g + 3 < GROUPS:
+                        load_fv(g + 3)
+                    if g < 3:
+                        load_wf(g + 1)
+                    else:
+                        load_w(g - 1)
+                    fv_quant(g)
+                    if g + 2 < GROUPS:
+                        fv_regroup(g + 2)
+                    if g + 1 < GROUPS:
+                        fv_transposes(g + 1, 0, 6)
+                    for n, ot in enumerate(EARLY):
+                        for c0 in (0, 512):
+                            if g == 0:
+                                acc = psum.tile([P, 512], F32, tag="bank", name="early")
+                                open_acc[(ot, c0)] = acc
+                            mx_pass(open_acc[(ot, c0)], ot, g, c0, 512)
+                        if g >= 2:
+                            gate_tile(2 * (g - 2) + n)
+                        if n == 0:
+                            if g + 1 < GROUPS:
+                                fv_transposes(g + 1, 6, PIX)
+                            if 1 <= g <= 4:
+                                gate_transposes(2 * (g - 1))
+                                gate_transposes(2 * (g - 1) + 1)
+                w_tile(2)
+                w_quant(2)
         pools["back"] = ctx.enter_context(tc.tile_pool(name="back", bufs=2))
-        ys = {}
-        for ot in range(OT):
-            ys[ot] = new_y(ot)
-            if ot < 2:
-                bn_relu(ys[ot], open_acc[(ot, 0)], ot, 0, 512, s_t, t_t)
-                bn_relu(ys[ot], open_acc[(ot, 512)], ot, 512, 512, s_t, t_t)
-                conv(ot, s_t, t_t, CHUNKS[2:], ys[ot])
-            else:
-                conv(ot, s_t, t_t, CHUNKS, ys[ot])
-            if ot >= 1:
-                finish(ot - 1, ys[ot - 1])
-        finish(OT - 1, ys[OT - 1])
+        load_w(5)
+        with tc.manual_schedule(engines={ENG.PE}):
+            ys = {}
+            for ot in range(OT):
+                ys[ot] = new_y(ot)
+                if ot < 2:
+                    bn_relu(ys[ot], open_acc[(ot, 0)], ot, 0, 512, s_t, t_t)
+                    bn_relu(ys[ot], open_acc[(ot, 512)], ot, 512, 512, s_t, t_t)
+                    conv(ot, s_t, t_t, CHUNKS[2:], ys[ot])
+                else:
+                    conv(ot, s_t, t_t, CHUNKS, ys[ot])
+                if 6 <= ot + 5 < OT:
+                    load_w(ot + 5)
+                if 3 <= ot + 2 < OT:
+                    w_tile(ot + 2)
+                    w_quant(ot + 2)
+                if ot >= 1:
+                    finish(ot - 1, ys[ot - 1])
+            finish(OT - 1, ys[OT - 1])

@@ -21,7 +21,7 @@ GROUPS = 6
 OT = 8
 COLS = PIX * B
 EPS = 1e-5
-FV_PARTS = (2, 1, 1, 1, 1, 1)
+FV_PARTS = (4, 1, 1, 1, 1, 1)
 FLOPS = 2 * C * C3 * COLS + 2 * B * C * C
 
 
@@ -128,17 +128,30 @@ def tile_joint_module_pa_kernel(tc, fv, ft, W1, b1, g1, be1, m1, v1, Wfc1, bfc1,
             )
 
         wgrs = {}
+        wsplit = {}
+
+        def w_split(ot):
+            wde = stage.tile([P, C3], BF16, tag="wde", bufs=2, name="wde%d" % ot)
+            nc.vector.tensor_copy(
+                out=wde[:].bitcast(F32).rearrange("o (g u q) -> o g u q", g=GROUPS, u=2, q=P),
+                in_=wraw[ot][:].bitcast(F32).rearrange("o (g q u) -> o g u q", g=GROUPS, q=P, u=2),
+            )
+            wsplit[ot] = wde
 
         def w_tile(ot):
-            words = wraw[ot][:].bitcast(F32)
+            split = ot in wsplit
+            words = (wsplit if split else wraw)[ot][:].bitcast(F32)
+            if split:
+                words = words.rearrange("o (g u q) -> o g u q", g=GROUPS, u=2, q=P)
+            else:
+                words = words.rearrange("o (g q u) -> o g u q", g=GROUPS, q=P, u=2)
             wgr = stage.tile([P, C3], BF16, tag="wgr", bufs=2, align_bytes=64, name="wgr%d" % ot)
             wv = wgr[:].bitcast(F32).rearrange("p (g o u) -> p g o u", g=GROUPS, o=P, u=2)
             for g0 in range(0, GROUPS, 2):
                 bank = psum.tile([P, 2, 2, P], F32, tag="bank", name="wbank")
                 for gg in range(2):
                     for u in range(2):
-                        k0 = 256 * (g0 + gg)
-                        nc.tensor.transpose(bank[:, gg, u, :], words[:, k0 + u : k0 + 256 : 2], ident_f[:])
+                        nc.tensor.transpose(bank[:, gg, u, :], words[:, g0 + gg, u, :], ident_f[:])
                 nc.scalar.copy(
                     out=wv[:, g0 : g0 + 2, :, :], in_=bank[:].rearrange("p g u o -> p g o u")
                 )
@@ -189,6 +202,8 @@ def tile_joint_module_pa_kernel(tc, fv, ft, W1, b1, g1, be1, m1, v1, Wfc1, bfc1,
             nc.scalar.copy(out=wft[:], in_=bank[:].rearrange("p k o -> p (k o)"))
             wfts[ot] = wft
 
+        gts = {}
+
         def gate_tile(ot):
             wv = wfts[ot][:].bitcast(BF16).rearrange("p (k o e) -> p k o e", k=4, o=P, e=2)
             fvw = ftT[:].bitcast(BF16).rearrange("p (k b e) -> p k b e", k=4, b=B, e=2)
@@ -202,9 +217,16 @@ def tile_joint_module_pa_kernel(tc, fv, ft, W1, b1, g1, be1, m1, v1, Wfc1, bfc1,
                         start=(kc == 0 and e == 0),
                         stop=(kc == 3 and e == 1),
                     )
-            gt = stage.tile([P, B], F32, tag="gt", bufs=2, align_bytes=64, name="gt")
-            nc.scalar.activation(out=gt[:], in_=acc[:], func=ACT.Identity, bias=bp1[:, ot : ot + 1], scale=1.0)
-            nc.vector.transpose(out=gate[:, ot * P : (ot + 1) * P], in_=gt[:])
+            if ot % 2 == 0:
+                gt = stage.tile([P, 2 * B], F32, tag="gt", bufs=2, align_bytes=64, name="gt%d" % ot)
+                gts[ot // 2] = gt
+            half = slice(ot % 2 * B, (ot % 2 + 1) * B)
+            nc.scalar.activation(
+                out=gts[ot // 2][:, half], in_=acc[:], func=ACT.Identity, bias=bp1[:, ot : ot + 1], scale=1.0
+            )
+
+        def gate_turn(i):
+            nc.vector.transpose(out=gate[:, 2 * i * P : 2 * (i + 1) * P], in_=gts[i][:])
 
         CHUNKS = ((0, 512), (512, 512), (1024, 128))
 
@@ -242,7 +264,7 @@ def tile_joint_module_pa_kernel(tc, fv, ft, W1, b1, g1, be1, m1, v1, Wfc1, bfc1,
         def finish(ot, y):
             last = ot == OT - 1
             yt = pools["back"].tile([P, COLS], F32, tag="yt", bufs=2, align_bytes=64, name="yt%d" % ot)
-            for c0, n in CHUNKS if last else ((0, 1024), (1024, 128)):
+            for c0, n in CHUNKS if last else ((1024, 128), (0, 1024)):
                 nc.vector.transpose(out=yt[:, c0 : c0 + n], in_=y[:, c0 : c0 + n])
             step = 2 if last else 4
             for j0 in range(0, 4, step):
@@ -264,72 +286,120 @@ def tile_joint_module_pa_kernel(tc, fv, ft, W1, b1, g1, be1, m1, v1, Wfc1, bfc1,
                         in_=osb[32 * i : 32 * i + 32, :, :].rearrange("l (j o) x -> l j (o x)", j=step),
                     )
 
-        EARLY = (0, 1)
+        open_acc = {}
+
+        def early(ot, g):
+            for c0 in (0, 512):
+                if g == 0:
+                    acc = psum.tile([P, 512], F32, tag="bank", name="early")
+                    open_acc[(ot, c0)] = acc
+                mx_pass(open_acc[(ot, c0)], ot, g, c0, 512)
+
+        pinned = {ENG.PE, ENG.DVE, ENG.Activation}
         with tc.tile_pool(name="front", bufs=2) as front:
             pools["front"] = front
-            load_fv(0)
-            load_w(0)
-            load_small()
-            load_fv(1)
-            load_w(1)
-            load_fv(2)
-            load_wf(0)
-            fv_regroup(0)
-            w_tile(0)
-            fv_regroup(1)
-            fv_transposes(0, 0, PIX)
-            w_quant(0)
-            w_tile(1)
-            s_t, t_t = params()
-            ft_transposes()
-            w_quant(1)
-            open_acc = {}
-            with tc.manual_schedule(engines={ENG.PE}):
-                for g in range(GROUPS):
-                    if g + 3 < GROUPS:
-                        load_fv(g + 3)
-                    if g < 3:
-                        load_wf(g + 1)
-                    else:
-                        load_w(g - 1)
-                    fv_quant(g)
-                    if g + 2 < GROUPS:
-                        fv_regroup(g + 2)
-                    if g + 1 < GROUPS:
-                        fv_transposes(g + 1, 0, 6)
-                    for n, ot in enumerate(EARLY):
-                        for c0 in (0, 512):
-                            if g == 0:
-                                acc = psum.tile([P, 512], F32, tag="bank", name="early")
-                                open_acc[(ot, c0)] = acc
-                            mx_pass(open_acc[(ot, c0)], ot, g, c0, 512)
-                        if g >= 2:
-                            gate_tile(2 * (g - 2) + n)
-                        if n == 0:
-                            if g + 1 < GROUPS:
-                                fv_transposes(g + 1, 6, PIX)
-                            if 1 <= g <= 4:
-                                gate_transposes(2 * (g - 1))
-                                gate_transposes(2 * (g - 1) + 1)
-                w_tile(2)
-                w_quant(2)
+            with tc.manual_schedule(engines=pinned):
+                load_fv(0)
+                load_fv(1)
+                load_w(0)
+                load_fv(2)
+                fv_regroup(0)
+                load_fv(3)
+                load_w(1)
+                load_small()
+                load_wf(0)
+                fv_regroup(1)
+                fv_transposes(0, 0, PIX)
+                w_tile(0)
+                fv_quant(0)
+                fv_regroup(2)
+                load_fv(4)
+                load_wf(1)
+                fv_transposes(1, 0, PIX)
+                w_quant(0)
+                load_wf(2)
+                fv_quant(1)
+                fv_regroup(3)
+                load_fv(5)
+                fv_transposes(2, 0, 6)
+                early(0, 0)
+                fv_transposes(2, 6, PIX)
+                w_tile(1)
+                early(0, 1)
+                fv_quant(2)
+                w_quant(1)
+                fv_regroup(4)
+                fv_transposes(3, 0, 6)
+                early(0, 2)
+                fv_transposes(3, 6, PIX)
+                for g in range(3):
+                    early(1, g)
+                ft_transposes()
+                gate_transposes(0)
+                gate_transposes(1)
+                fv_quant(3)
+                fv_regroup(5)
+                load_wf(3)
+                fv_transposes(4, 0, 6)
+                early(0, 3)
+                fv_transposes(4, 6, PIX)
+                s_t, t_t = params()
+                gate_transposes(2)
+                gate_transposes(3)
+                gate_tile(0)
+                early(1, 3)
+                gate_tile(1)
+                load_w(2)
+                load_w(3)
+                fv_quant(4)
+                w_split(2)
+                gate_turn(0)
+                fv_transposes(5, 0, 6)
+                gate_tile(2)
+                fv_transposes(5, 6, PIX)
+                gate_transposes(4)
+                gate_transposes(5)
+                early(0, 4)
+                gate_tile(3)
+                early(1, 4)
+                w_split(3)
+                load_w(4)
+                fv_quant(5)
         pools["back"] = ctx.enter_context(tc.tile_pool(name="back", bufs=2))
-        load_w(5)
-        with tc.manual_schedule(engines={ENG.PE}):
-            ys = {}
-            for ot in range(OT):
+        ys = {}
+        with tc.manual_schedule(engines=pinned):
+            gate_transposes(6)
+            gate_transposes(7)
+            w_tile(2)
+            gate_tile(4)
+            gate_tile(5)
+            for ot in range(2):
                 ys[ot] = new_y(ot)
-                if ot < 2:
-                    bn_relu(ys[ot], open_acc[(ot, 0)], ot, 0, 512, s_t, t_t)
-                    bn_relu(ys[ot], open_acc[(ot, 512)], ot, 512, 512, s_t, t_t)
-                    conv(ot, s_t, t_t, CHUNKS[2:], ys[ot])
-                else:
-                    conv(ot, s_t, t_t, CHUNKS, ys[ot])
-                if 6 <= ot + 5 < OT:
-                    load_w(ot + 5)
-                if 3 <= ot + 2 < OT:
+                early(ot, 5)
+                bn_relu(ys[ot], open_acc[(ot, 0)], ot, 0, 512, s_t, t_t)
+                bn_relu(ys[ot], open_acc[(ot, 512)], ot, 512, 512, s_t, t_t)
+                conv(ot, s_t, t_t, CHUNKS[2:], ys[ot])
+            gate_turn(1)
+            w_quant(2)
+            gate_tile(6)
+            gate_tile(7)
+            load_w(5)
+            w_tile(3)
+            finish(0, ys[0])
+            w_split(4)
+            gate_turn(2)
+            w_quant(3)
+            gate_turn(3)
+            for ot in range(2, OT):
+                ys[ot] = new_y(ot)
+                conv(ot, s_t, t_t, CHUNKS, ys[ot])
+                if ot + 4 < OT:
+                    load_w(ot + 4)
+                if ot + 2 < OT:
                     w_tile(ot + 2)
+                finish(ot - 1, ys[ot - 1])
+                if ot + 3 < OT:
+                    w_split(ot + 3)
+                if ot + 2 < OT:
                     w_quant(ot + 2)
-                if ot >= 1:
-                    finish(ot - 1, ys[ot - 1])
             finish(OT - 1, ys[OT - 1])

@@ -22,6 +22,7 @@ OT = 8
 COLS = PIX * B
 EPS = 1e-5
 FV_PARTS = (4, 1, 1, 1, 1, 1)
+ON_TENSOR = (1, 3, 5, 7)
 FLOPS = 2 * C * C3 * COLS + 2 * B * C * C
 
 
@@ -34,7 +35,8 @@ def tile_joint_module_pa_kernel(tc, fv, ft, W1, b1, g1, be1, m1, v1, Wfc1, bfc1,
         psum = ctx.enter_context(tc.psum_pool(name="psum", bufs=8))
 
         fv_flat = fv.rearrange("b c h w -> b (c h w)")
-        out_rows = out.rearrange("b o h w -> b (o h w)").rearrange("(j l) f -> l j f", l=32)
+        out_flat = out.rearrange("b o h w -> b (o h w)")
+        out_rows = out_flat.rearrange("(j l) f -> l j f", l=32)
         wfc_view = Wfc1.rearrange("(t p) k -> p t k", p=P)
 
         ptile = const.tile([P, P], BF16)
@@ -226,7 +228,16 @@ def tile_joint_module_pa_kernel(tc, fv, ft, W1, b1, g1, be1, m1, v1, Wfc1, bfc1,
             )
 
         def gate_turn(i):
-            nc.vector.transpose(out=gate[:, 2 * i * P : 2 * (i + 1) * P], in_=gts[i][:])
+            todo = [ot for ot in (2 * i, 2 * i + 1) if ot not in ON_TENSOR]
+            c0 = (todo[0] - 2 * i) * B
+            c1 = c0 + len(todo) * B
+            nc.vector.transpose(out=gate[:, 2 * i * P + c0 : 2 * i * P + c1], in_=gts[i][:, c0:c1])
+            for ot in (2 * i, 2 * i + 1):
+                if ot in ON_TENSOR:
+                    bank = psum.tile([P, P], F32, tag="bank", name="gtbank")
+                    half = slice(ot % 2 * B, (ot % 2 + 1) * B)
+                    nc.tensor.transpose(bank[:], gts[i][:, half], ident_f[:])
+                    nc.scalar.copy(out=gate[:, ot * P : (ot + 1) * P], in_=bank[:])
 
         CHUNKS = ((0, 512), (512, 512), (1024, 128))
 
@@ -261,30 +272,59 @@ def tile_joint_module_pa_kernel(tc, fv, ft, W1, b1, g1, be1, m1, v1, Wfc1, bfc1,
             y = pools["back"].tile([P, COLS], F32, tag="y", bufs=3, align_bytes=64, name="y%d" % ot)
             return y
 
-        def finish(ot, y):
-            last = ot == OT - 1
-            yt = pools["back"].tile([P, COLS], F32, tag="yt", bufs=2, align_bytes=64, name="yt%d" % ot)
-            for c0, n in CHUNKS if last else ((1024, 128), (0, 1024)):
-                nc.vector.transpose(out=yt[:, c0 : c0 + n], in_=y[:, c0 : c0 + n])
-            step = 2 if last else 4
-            for j0 in range(0, 4, step):
-                osb = pools["back"].tile([P, 32 * step, PIX], F32, tag="osb", bufs=4, name="osb%d" % ot)
-                nn = 8 * step
+        planes = {}
+
+        def turn(ot, y, c):
+            c0, n = CHUNKS[c]
+            if c == 0:
+                pl = pools["back"].tile([P, PIX, P], F32, tag="yt", bufs=2, align_bytes=64, name="planes%d" % ot)
+                planes[ot] = pl
+            x0, nx = c0 // B, n // B
+            z = psum.tile([P, nx, P], F32, tag="bank", name="z")
+            for i in range(nx):
+                nc.tensor.transpose(z[:, i, :], y[:, (x0 + i) * B : (x0 + i + 1) * B], ident_f[:])
+            nc.scalar.copy(out=planes[ot][:, x0 : x0 + nx, :], in_=z[:])
+
+        def finish_turned(ot):
+            for i0 in (0, 64):
+                osb = pools["back"].tile([P, 64, PIX], F32, tag="osb", bufs=4, name="osb%d" % ot)
+                o0 = ot * P + i0
                 nc.vector.tensor_tensor(
-                    out=osb[:].rearrange("p (n i) x -> p n x i", i=4),
-                    in0=yt[:].rearrange("p (x n i) -> p n x i", x=PIX, i=4)[:, 8 * j0 : 8 * j0 + nn, :, :],
-                    in1=gate[:, ot * P + 32 * j0 : ot * P + 32 * (j0 + step)]
-                    .rearrange("p (n i) -> p n i", i=4)
+                    out=osb[:].rearrange("b (n i) x -> b n x i", i=4),
+                    in0=planes[ot][:, :, i0 : i0 + 64].rearrange("b x (n i) -> b n x i", i=4),
+                    in1=gate[:, o0 : o0 + 64]
+                    .rearrange("b (n i) -> b n i", i=4)
                     .unsqueeze(2)
-                    .to_broadcast([P, nn, PIX, 4]),
+                    .to_broadcast([P, 16, PIX, 4]),
                     op=ALU.mult,
                 )
-                for i in range(4):
-                    f0 = (ot * P + 32 * i) * PIX
-                    nc.sync.dma_start(
-                        out=out_rows[:, j0 : j0 + step, f0 : f0 + 32 * PIX],
-                        in_=osb[32 * i : 32 * i + 32, :, :].rearrange("l (j o) x -> l j (o x)", j=step),
-                    )
+                nc.sync.dma_start(
+                    out=out_flat[:, o0 * PIX : (o0 + 64) * PIX], in_=osb[:].rearrange("b o x -> b (o x)")
+                )
+
+        def finish(ot, y):
+            if ot in ON_TENSOR:
+                finish_turned(ot)
+                return
+            yt = pools["back"].tile([P, COLS], F32, tag="yt", bufs=2, align_bytes=64, name="yt%d" % ot)
+            nc.vector.transpose(out=yt[:, 1024:1152], in_=y[:, 1024:1152])
+            nc.vector.transpose(out=yt[:, 0:1024], in_=y[:, 0:1024])
+            osb = pools["back"].tile([P, P, PIX], F32, tag="osb", bufs=4, name="osb%d" % ot)
+            nc.vector.tensor_tensor(
+                out=osb[:].rearrange("p (n i) x -> p n x i", i=4),
+                in0=yt[:].rearrange("p (x n i) -> p n x i", x=PIX, i=4),
+                in1=gate[:, ot * P : (ot + 1) * P]
+                .rearrange("p (n i) -> p n i", i=4)
+                .unsqueeze(2)
+                .to_broadcast([P, P // 4, PIX, 4]),
+                op=ALU.mult,
+            )
+            for i in range(4):
+                f0 = (ot * P + 32 * i) * PIX
+                nc.sync.dma_start(
+                    out=out_rows[:, :, f0 : f0 + 32 * PIX],
+                    in_=osb[32 * i : 32 * i + 32, :, :].rearrange("l (j o) x -> l j (o x)", j=4),
+                )
 
         open_acc = {}
 
@@ -385,6 +425,8 @@ def tile_joint_module_pa_kernel(tc, fv, ft, W1, b1, g1, be1, m1, v1, Wfc1, bfc1,
             gate_tile(7)
             load_w(5)
             w_tile(3)
+            for c in range(3):
+                turn(1, ys[1], c)
             finish(0, ys[0])
             w_split(4)
             gate_turn(2)
@@ -392,11 +434,21 @@ def tile_joint_module_pa_kernel(tc, fv, ft, W1, b1, g1, be1, m1, v1, Wfc1, bfc1,
             gate_turn(3)
             for ot in range(2, OT):
                 ys[ot] = new_y(ot)
-                conv(ot, s_t, t_t, CHUNKS, ys[ot])
+                if ot == OT - 1:
+                    conv(ot, s_t, t_t, CHUNKS[0:2], ys[ot])
+                    turn(ot, ys[ot], 0)
+                    conv(ot, s_t, t_t, CHUNKS[2:], ys[ot])
+                    turn(ot, ys[ot], 1)
+                    turn(ot, ys[ot], 2)
+                else:
+                    conv(ot, s_t, t_t, CHUNKS, ys[ot])
                 if ot + 4 < OT:
                     load_w(ot + 4)
                 if ot + 2 < OT:
                     w_tile(ot + 2)
+                if ot in ON_TENSOR and ot < OT - 1:
+                    for c in range(3):
+                        turn(ot, ys[ot], c)
                 finish(ot - 1, ys[ot - 1])
                 if ot + 3 < OT:
                     w_split(ot + 3)

@@ -21,8 +21,8 @@ GROUPS = 6
 OT = 8
 COLS = PIX * B
 EPS = 1e-5
-FV_PARTS = (4, 1, 1, 1, 1, 1)
-ON_TENSOR = (1, 3, 5, 7)
+FV_PARTS = (4, 2, 1, 1, 1, 1)
+ON_TENSOR = (4, 6, 7)
 FLOPS = 2 * C * C3 * COLS + 2 * B * C * C
 
 
@@ -228,18 +228,21 @@ def tile_joint_module_pa_kernel(tc, fv, ft, W1, b1, g1, be1, m1, v1, Wfc1, bfc1,
             )
 
         def gate_turn(i):
-            todo = [ot for ot in (2 * i, 2 * i + 1) if ot not in ON_TENSOR]
-            c0 = (todo[0] - 2 * i) * B
-            c1 = c0 + len(todo) * B
-            nc.vector.transpose(out=gate[:, 2 * i * P + c0 : 2 * i * P + c1], in_=gts[i][:, c0:c1])
-            for ot in (2 * i, 2 * i + 1):
+            pair = (2 * i, 2 * i + 1)
+            if not any(ot in ON_TENSOR for ot in pair):
+                nc.vector.transpose(out=gate[:, 2 * i * P : 2 * (i + 1) * P], in_=gts[i][:])
+                return
+            for ot in pair:
+                half = slice(ot % 2 * B, (ot % 2 + 1) * B)
                 if ot in ON_TENSOR:
                     bank = psum.tile([P, P], F32, tag="bank", name="gtbank")
-                    half = slice(ot % 2 * B, (ot % 2 + 1) * B)
                     nc.tensor.transpose(bank[:], gts[i][:, half], ident_f[:])
                     nc.scalar.copy(out=gate[:, ot * P : (ot + 1) * P], in_=bank[:])
+                else:
+                    nc.vector.transpose(out=gate[:, ot * P : (ot + 1) * P], in_=gts[i][:, half])
 
         CHUNKS = ((0, 512), (512, 512), (1024, 128))
+        LAST = ((1024, 128), (0, 512), (512, 256), (768, 256))
 
         def mx_pass(acc, ot, g, c0, n):
             nc.tensor.matmul_mx(
@@ -274,41 +277,46 @@ def tile_joint_module_pa_kernel(tc, fv, ft, W1, b1, g1, be1, m1, v1, Wfc1, bfc1,
 
         planes = {}
 
-        def turn(ot, y, c):
-            c0, n = CHUNKS[c]
-            if c == 0:
+        def turn(ot, y, chunks, copy=nc.scalar.copy):
+            if ot not in planes:
                 pl = pools["back"].tile([P, PIX, P], F32, tag="yt", bufs=2, align_bytes=64, name="planes%d" % ot)
                 planes[ot] = pl
-            x0, nx = c0 // B, n // B
-            z = psum.tile([P, nx, P], F32, tag="bank", name="z")
-            for i in range(nx):
-                nc.tensor.transpose(z[:, i, :], y[:, (x0 + i) * B : (x0 + i + 1) * B], ident_f[:])
-            nc.scalar.copy(out=planes[ot][:, x0 : x0 + nx, :], in_=z[:])
+            for c0, n in chunks:
+                x0, nx = c0 // B, n // B
+                z = psum.tile([P, nx, P], F32, tag="bank", name="z")
+                for i in range(nx):
+                    nc.tensor.transpose(z[:, i, :], y[:, (x0 + i) * B : (x0 + i + 1) * B], ident_f[:])
+                copy(out=planes[ot][:, x0 : x0 + nx, :], in_=z[:])
 
         def finish_turned(ot):
-            for i0 in (0, 64):
-                osb = pools["back"].tile([P, 64, PIX], F32, tag="osb", bufs=4, name="osb%d" % ot)
+            step = 32 if ot == OT - 1 else 64
+            for i0 in range(0, P, step):
+                osb = pools["back"].tile([P, step, PIX], F32, tag="osb", bufs=4, name="osb%d" % ot)
                 o0 = ot * P + i0
                 nc.vector.tensor_tensor(
                     out=osb[:].rearrange("b (n i) x -> b n x i", i=4),
-                    in0=planes[ot][:, :, i0 : i0 + 64].rearrange("b x (n i) -> b n x i", i=4),
-                    in1=gate[:, o0 : o0 + 64]
+                    in0=planes[ot][:, :, i0 : i0 + step].rearrange("b x (n i) -> b n x i", i=4),
+                    in1=gate[:, o0 : o0 + step]
                     .rearrange("b (n i) -> b n i", i=4)
                     .unsqueeze(2)
-                    .to_broadcast([P, 16, PIX, 4]),
+                    .to_broadcast([P, step // 4, PIX, 4]),
                     op=ALU.mult,
                 )
                 nc.sync.dma_start(
-                    out=out_flat[:, o0 * PIX : (o0 + 64) * PIX], in_=osb[:].rearrange("b o x -> b (o x)")
+                    out=out_flat[:, o0 * PIX : (o0 + step) * PIX], in_=osb[:].rearrange("b o x -> b (o x)")
                 )
 
-        def finish(ot, y):
+        def finish(ot, y, between=None):
             if ot in ON_TENSOR:
                 finish_turned(ot)
+                if between is not None:
+                    between()
                 return
             yt = pools["back"].tile([P, COLS], F32, tag="yt", bufs=2, align_bytes=64, name="yt%d" % ot)
             nc.vector.transpose(out=yt[:, 1024:1152], in_=y[:, 1024:1152])
             nc.vector.transpose(out=yt[:, 0:1024], in_=y[:, 0:1024])
+            if between is not None:
+                between()
             osb = pools["back"].tile([P, P, PIX], F32, tag="osb", bufs=4, name="osb%d" % ot)
             nc.vector.tensor_tensor(
                 out=osb[:].rearrange("p (n i) x -> p n x i", i=4),
@@ -402,7 +410,6 @@ def tile_joint_module_pa_kernel(tc, fv, ft, W1, b1, g1, be1, m1, v1, Wfc1, bfc1,
                 early(0, 4)
                 gate_tile(3)
                 early(1, 4)
-                w_split(3)
                 load_w(4)
                 fv_quant(5)
         pools["back"] = ctx.enter_context(tc.tile_pool(name="back", bufs=2))
@@ -411,35 +418,32 @@ def tile_joint_module_pa_kernel(tc, fv, ft, W1, b1, g1, be1, m1, v1, Wfc1, bfc1,
             gate_transposes(6)
             gate_transposes(7)
             w_tile(2)
-            gate_tile(4)
-            gate_tile(5)
             for ot in range(2):
                 ys[ot] = new_y(ot)
                 early(ot, 5)
                 bn_relu(ys[ot], open_acc[(ot, 0)], ot, 0, 512, s_t, t_t)
                 bn_relu(ys[ot], open_acc[(ot, 512)], ot, 512, 512, s_t, t_t)
                 conv(ot, s_t, t_t, CHUNKS[2:], ys[ot])
+            w_split(3)
             gate_turn(1)
             w_quant(2)
+            gate_tile(4)
+            gate_tile(5)
             gate_tile(6)
             gate_tile(7)
             load_w(5)
             w_tile(3)
-            for c in range(3):
-                turn(1, ys[1], c)
-            finish(0, ys[0])
-            w_split(4)
+            finish(0, ys[0], lambda: w_split(4))
             gate_turn(2)
             w_quant(3)
             gate_turn(3)
             for ot in range(2, OT):
                 ys[ot] = new_y(ot)
                 if ot == OT - 1:
-                    conv(ot, s_t, t_t, CHUNKS[0:2], ys[ot])
-                    turn(ot, ys[ot], 0)
-                    conv(ot, s_t, t_t, CHUNKS[2:], ys[ot])
-                    turn(ot, ys[ot], 1)
-                    turn(ot, ys[ot], 2)
+                    conv(ot, s_t, t_t, LAST, ys[ot])
+                    finish(ot - 1, ys[ot - 1])
+                    turn(ot, ys[ot], LAST[0:2], nc.vector.tensor_copy)
+                    turn(ot, ys[ot], LAST[2:])
                 else:
                     conv(ot, s_t, t_t, CHUNKS, ys[ot])
                 if ot + 4 < OT:
@@ -447,11 +451,11 @@ def tile_joint_module_pa_kernel(tc, fv, ft, W1, b1, g1, be1, m1, v1, Wfc1, bfc1,
                 if ot + 2 < OT:
                     w_tile(ot + 2)
                 if ot in ON_TENSOR and ot < OT - 1:
-                    for c in range(3):
-                        turn(ot, ys[ot], c)
-                finish(ot - 1, ys[ot - 1])
+                    turn(ot, ys[ot], CHUNKS)
                 if ot + 3 < OT:
-                    w_split(ot + 3)
+                    finish(ot - 1, ys[ot - 1], lambda: w_split(ot + 3))
+                elif ot < OT - 1:
+                    finish(ot - 1, ys[ot - 1])
                 if ot + 2 < OT:
                     w_quant(ot + 2)
             finish(OT - 1, ys[OT - 1])

@@ -22,7 +22,7 @@ OT = 8
 COLS = PIX * B
 EPS = 1e-5
 FV_PARTS = (4, 2, 1, 1, 1, 1)
-ON_TENSOR = (4, 6, 7)
+ON_TENSOR = (6, 7)
 FLOPS = 2 * C * C3 * COLS + 2 * B * C * C
 
 
@@ -55,10 +55,10 @@ def tile_joint_module_pa_kernel(tc, fv, ft, W1, b1, g1, be1, m1, v1, Wfc1, bfc1,
                 nc.sync.dma_start(out=ptile[8 * v : 8 * v + 8, :], in_=vec.rearrange("(t p) -> t p", p=P))
             nc.sync.dma_start(out=ftraw[:], in_=ft)
 
-        fvc = keep.tile([P, GROUPS, COLS], U32, align_bytes=64)
-        fvs = keep.tile([P, GROUPS, COLS], U8, align_bytes=64)
-        w1c = keep.tile([P, OT, GROUPS * P], U32, align_bytes=64)
-        w1s = keep.tile([P, OT, GROUPS * P], U8, align_bytes=64)
+        fvc = keep.tile([P, GROUPS, COLS], U32, align_bytes=256)
+        fvs = keep.tile([P, GROUPS, COLS], U8, align_bytes=256)
+        w1c = keep.tile([P, OT, GROUPS * P], U32, align_bytes=256)
+        w1s = keep.tile([P, OT, GROUPS * P], U8, align_bytes=256)
         ftT = keep.tile([P, 4 * B], F32)
         gate = keep.tile([P, C], F32, align_bytes=64)
         bp1 = keep.tile([P, OT], F32)
@@ -133,8 +133,9 @@ def tile_joint_module_pa_kernel(tc, fv, ft, W1, b1, g1, be1, m1, v1, Wfc1, bfc1,
         wsplit = {}
 
         def w_split(ot):
+            copy = nc.scalar.copy if ot in (5, 7) else nc.vector.tensor_copy
             wde = stage.tile([P, C3], BF16, tag="wde", bufs=2, name="wde%d" % ot)
-            nc.vector.tensor_copy(
+            copy(
                 out=wde[:].bitcast(F32).rearrange("o (g u q) -> o g u q", g=GROUPS, u=2, q=P),
                 in_=wraw[ot][:].bitcast(F32).rearrange("o (g q u) -> o g u q", g=GROUPS, q=P, u=2),
             )
@@ -275,6 +276,12 @@ def tile_joint_module_pa_kernel(tc, fv, ft, W1, b1, g1, be1, m1, v1, Wfc1, bfc1,
             y = pools["back"].tile([P, COLS], F32, tag="y", bufs=3, align_bytes=64, name="y%d" % ot)
             return y
 
+        def w_next(ot):
+            if ot + 3 < OT:
+                w_split(ot + 3)
+            if ot + 2 < OT:
+                w_quant(ot + 2)
+
         planes = {}
 
         def turn(ot, y, chunks, copy=nc.scalar.copy):
@@ -294,12 +301,12 @@ def tile_joint_module_pa_kernel(tc, fv, ft, W1, b1, g1, be1, m1, v1, Wfc1, bfc1,
                 osb = pools["back"].tile([P, step, PIX], F32, tag="osb", bufs=4, name="osb%d" % ot)
                 o0 = ot * P + i0
                 nc.vector.tensor_tensor(
-                    out=osb[:].rearrange("b (n i) x -> b n x i", i=4),
-                    in0=planes[ot][:, :, i0 : i0 + step].rearrange("b x (n i) -> b n x i", i=4),
+                    out=osb[:].rearrange("b (n i) x -> b n x i", i=2),
+                    in0=planes[ot][:, :, i0 : i0 + step].rearrange("b x (n i) -> b n x i", i=2),
                     in1=gate[:, o0 : o0 + step]
-                    .rearrange("b (n i) -> b n i", i=4)
+                    .rearrange("b (n i) -> b n i", i=2)
                     .unsqueeze(2)
-                    .to_broadcast([P, step // 4, PIX, 4]),
+                    .to_broadcast([P, step // 2, PIX, 2]),
                     op=ALU.mult,
                 )
                 nc.sync.dma_start(
@@ -308,9 +315,9 @@ def tile_joint_module_pa_kernel(tc, fv, ft, W1, b1, g1, be1, m1, v1, Wfc1, bfc1,
 
         def finish(ot, y, between=None):
             if ot in ON_TENSOR:
-                finish_turned(ot)
                 if between is not None:
                     between()
+                finish_turned(ot)
                 return
             yt = pools["back"].tile([P, COLS], F32, tag="yt", bufs=2, align_bytes=64, name="yt%d" % ot)
             nc.vector.transpose(out=yt[:, 1024:1152], in_=y[:, 1024:1152])
@@ -319,12 +326,12 @@ def tile_joint_module_pa_kernel(tc, fv, ft, W1, b1, g1, be1, m1, v1, Wfc1, bfc1,
                 between()
             osb = pools["back"].tile([P, P, PIX], F32, tag="osb", bufs=4, name="osb%d" % ot)
             nc.vector.tensor_tensor(
-                out=osb[:].rearrange("p (n i) x -> p n x i", i=4),
-                in0=yt[:].rearrange("p (x n i) -> p n x i", x=PIX, i=4),
+                out=osb[:].rearrange("p (n i) x -> p n x i", i=2),
+                in0=yt[:].rearrange("p (x n i) -> p n x i", x=PIX, i=2),
                 in1=gate[:, ot * P : (ot + 1) * P]
-                .rearrange("p (n i) -> p n i", i=4)
+                .rearrange("p (n i) -> p n i", i=2)
                 .unsqueeze(2)
-                .to_broadcast([P, P // 4, PIX, 4]),
+                .to_broadcast([P, P // 2, PIX, 2]),
                 op=ALU.mult,
             )
             for i in range(4):
@@ -433,9 +440,8 @@ def tile_joint_module_pa_kernel(tc, fv, ft, W1, b1, g1, be1, m1, v1, Wfc1, bfc1,
             gate_tile(7)
             load_w(5)
             w_tile(3)
-            finish(0, ys[0], lambda: w_split(4))
+            finish(0, ys[0], lambda: w_next(1))
             gate_turn(2)
-            w_quant(3)
             gate_turn(3)
             for ot in range(2, OT):
                 ys[ot] = new_y(ot)
@@ -452,10 +458,6 @@ def tile_joint_module_pa_kernel(tc, fv, ft, W1, b1, g1, be1, m1, v1, Wfc1, bfc1,
                     w_tile(ot + 2)
                 if ot in ON_TENSOR and ot < OT - 1:
                     turn(ot, ys[ot], CHUNKS)
-                if ot + 3 < OT:
-                    finish(ot - 1, ys[ot - 1], lambda: w_split(ot + 3))
-                elif ot < OT - 1:
-                    finish(ot - 1, ys[ot - 1])
-                if ot + 2 < OT:
-                    w_quant(ot + 2)
+                if ot < OT - 1:
+                    finish(ot - 1, ys[ot - 1], lambda: w_next(ot))
             finish(OT - 1, ys[OT - 1])

from contextlib import ExitStack

import concourse.mybir as mybir
from concourse.masks import make_identity

F32 = mybir.dt.float32
BF16 = mybir.dt.bfloat16
U32 = mybir.dt.uint32
U8 = mybir.dt.uint8
FP8X4 = mybir.dt.float8_e4m3fn_x4
ACT = mybir.ActivationFunctionType
ALU = mybir.AluOpType
ENG = mybir.EngineType

P = 128
B = 128
C = 1024
C3 = 3072
PIX = 9
GROUPS = 6
OT = 8
COLS = PIX * B
EPS = 1e-5
FV_PARTS = (4, 2, 1, 1, 1, 1)
ON_TENSOR = (6, 7)
FLOPS = 2 * C * C3 * COLS + 2 * B * C * C


def tile_joint_module_pa_kernel(tc, fv, ft, W1, b1, g1, be1, m1, v1, Wfc1, bfc1, out):
    nc = tc.nc
    with ExitStack() as ctx:
        const = ctx.enter_context(tc.tile_pool(name="const", bufs=1))
        keep = ctx.enter_context(tc.tile_pool(name="keep", bufs=1))
        stage = ctx.enter_context(tc.tile_pool(name="stage", bufs=2))
        psum = ctx.enter_context(tc.psum_pool(name="psum", bufs=8))

        fv_flat = fv.rearrange("b c h w -> b (c h w)")
        out_flat = out.rearrange("b o h w -> b (o h w)")
        out_rows = out_flat.rearrange("(j l) f -> l j f", l=32)
        wfc_view = Wfc1.rearrange("(t p) k -> p t k", p=P)

        ptile = const.tile([P, P], BF16)
        ftraw = const.tile([P, C], BF16)
        warm = const.tile([P, 1], F32)
        nc.vector.memset(warm[:], 1.0)
        nc.scalar.sqrt(out=warm[:], in_=warm[:])
        ident_f = const.tile([P, P], F32)
        make_identity(nc, ident_f[:])
        nc.gpsimd.memset(ptile[:], 0.0)
        ident_b = const.tile([P, P], BF16)
        make_identity(nc, ident_b[:])

        def load_small():
            for v, vec in enumerate((b1, g1, be1, m1, v1, bfc1)):
                nc.sync.dma_start(out=ptile[8 * v : 8 * v + 8, :], in_=vec.rearrange("(t p) -> t p", p=P))
            nc.sync.dma_start(out=ftraw[:], in_=ft)

        fvc = keep.tile([P, GROUPS, COLS], U32, align_bytes=256)
        fvs = keep.tile([P, GROUPS, COLS], U8, align_bytes=256)
        w1c = keep.tile([P, OT, GROUPS * P], U32, align_bytes=256)
        w1s = keep.tile([P, OT, GROUPS * P], U8, align_bytes=256)
        ftT = keep.tile([P, 4 * B], F32)
        gate = keep.tile([P, C], F32, align_bytes=64)
        bp1 = keep.tile([P, OT], F32)

        pools = {}
        fvraw = {}
        wraw = {}
        wfraw = {}

        def load_fv(g):
            raw = pools["front"].tile([P, 512 * PIX], BF16, tag="fvraw", bufs=3, name="fvraw%d" % g)
            part = 4608 // FV_PARTS[g]
            for c in range(0, 4608, part):
                nc.sync.dma_start(
                    out=raw[:, c : c + part], in_=fv_flat[:, g * 4608 + c : g * 4608 + c + part]
                )
            fvraw[g] = raw

        def load_w(ot):
            raw = stage.tile([P, C3], BF16, tag="wraw", bufs=4, name="wraw%d" % ot)
            nc.sync.dma_start(out=raw[:], in_=W1[ot * P : (ot + 1) * P, :])
            wraw[ot] = raw

        def load_wf(i):
            raw = stage.tile([P, 2, C], BF16, tag="wfraw", bufs=4, name="wfraw%d" % i)
            nc.sync.dma_start(out=raw[:], in_=wfc_view[:, 2 * i : 2 * i + 2, :])
            wfraw[i] = raw

        pres = {}
        grs = {}

        def fv_regroup(g):
            src = fvraw[g][:].rearrange("b (p u e x) -> b u p e x", p=P, u=2, e=2, x=PIX)
            pre = pools["front"].tile([P, PIX * 512], BF16, tag="pre", bufs=2, name="pre%d" % g)
            dst = pre[:].rearrange("b (x u p e) -> b u p e x", x=PIX, u=2, p=P, e=2)
            part = P // FV_PARTS[g]
            for p0 in range(0, P, part):
                for x0 in range(0, PIX, 3):
                    nc.vector.tensor_copy(
                        out=dst[:, :, p0 : p0 + part, :, x0 : x0 + 3],
                        in_=src[:, :, p0 : p0 + part, :, x0 : x0 + 3],
                    )
            pres[g] = pre

        def fv_transposes(g, x_from, x_to):
            words = pres[g][:].bitcast(F32).rearrange("b (x u p) -> b x u p", x=PIX, u=2, p=P)
            if g not in grs:
                gr = pools["front"].tile([P, PIX * 512], BF16, tag="gr", bufs=2, align_bytes=64, name="gr%d" % g)
                grs[g] = gr
            grw = grs[g][:].bitcast(F32).rearrange("p (x b u) -> p x b u", x=PIX, b=B, u=2)
            for x0 in range(x_from, x_to, 2):
                nx = min(2, x_to - x0)
                bank = psum.tile([P, 2, 2, B], F32, tag="bank", name="fvbank")
                for x in range(nx):
                    for u in range(2):
                        nc.tensor.transpose(bank[:, x, u, :], words[:, x0 + x, u, :], ident_f[:])
                nc.scalar.copy(
                    out=grw[:, x0 : x0 + nx, :, :],
                    in_=bank[:, 0:nx, :, :].rearrange("p x u b -> p x b u"),
                )

        def fv_quant(g):
            gr = grs[g]
            nc.vector.quantize_mx(
                out=fvc[:, g, 0:1024].bitcast(FP8X4), scales=fvs[:, g, 0:1024], in_=gr[:, 0:4096]
            )
            nc.vector.quantize_mx(
                out=fvc[:, g, 1024:1152].bitcast(FP8X4), scales=fvs[:, g, 1024:1152], in_=gr[:, 4096:4608]
            )

        wgrs = {}
        wsplit = {}

        def w_split(ot):
            copy = nc.scalar.copy if ot in (5, 7) else nc.vector.tensor_copy
            wde = stage.tile([P, C3], BF16, tag="wde", bufs=2, name="wde%d" % ot)
            copy(
                out=wde[:].bitcast(F32).rearrange("o (g u q) -> o g u q", g=GROUPS, u=2, q=P),
                in_=wraw[ot][:].bitcast(F32).rearrange("o (g q u) -> o g u q", g=GROUPS, q=P, u=2),
            )
            wsplit[ot] = wde

        def w_tile(ot):
            split = ot in wsplit
            words = (wsplit if split else wraw)[ot][:].bitcast(F32)
            if split:
                words = words.rearrange("o (g u q) -> o g u q", g=GROUPS, u=2, q=P)
            else:
                words = words.rearrange("o (g q u) -> o g u q", g=GROUPS, q=P, u=2)
            wgr = stage.tile([P, C3], BF16, tag="wgr", bufs=2, align_bytes=64, name="wgr%d" % ot)
            wv = wgr[:].bitcast(F32).rearrange("p (g o u) -> p g o u", g=GROUPS, o=P, u=2)
            for g0 in range(0, GROUPS, 2):
                bank = psum.tile([P, 2, 2, P], F32, tag="bank", name="wbank")
                for gg in range(2):
                    for u in range(2):
                        nc.tensor.transpose(bank[:, gg, u, :], words[:, g0 + gg, u, :], ident_f[:])
                nc.scalar.copy(
                    out=wv[:, g0 : g0 + 2, :, :], in_=bank[:].rearrange("p g u o -> p g o u")
                )
            wgrs[ot] = wgr

        def w_quant(ot):
            wgr = wgrs[ot]
            nc.vector.quantize_mx(
                out=w1c[:, ot, 0:512].bitcast(FP8X4), scales=w1s[:, ot, 0:512], in_=wgr[:, 0:2048]
            )
            nc.vector.quantize_mx(
                out=w1c[:, ot, 512:768].bitcast(FP8X4), scales=w1s[:, ot, 512:768], in_=wgr[:, 2048:3072]
            )

        def params():
            pbank = psum.tile([P, P], BF16, tag="bank", name="pbank")
            nc.tensor.transpose(pbank[:], ptile[:], ident_b[:])
            prm = const.tile([P, 48], F32)
            nc.vector.tensor_copy(out=prm[:], in_=pbank[:, 0:48])
            nc.vector.tensor_scalar_add(out=bp1[:], in0=prm[:, 40:48], scalar1=1.0)
            s_t = const.tile([P, OT], F32)
            t_t = const.tile([P, OT], F32)
            tmp = const.tile([P, OT], F32)
            nc.vector.tensor_scalar_add(out=tmp[:], in0=prm[:, 32:40], scalar1=EPS)
            nc.scalar.sqrt(out=tmp[:], in_=tmp[:])
            nc.vector.reciprocal(out=tmp[:], in_=tmp[:])
            nc.vector.tensor_mul(out=s_t[:], in0=prm[:, 8:16], in1=tmp[:])
            nc.vector.tensor_sub(out=t_t[:], in0=prm[:, 0:8], in1=prm[:, 24:32])
            nc.vector.tensor_mul(out=t_t[:], in0=t_t[:], in1=s_t[:])
            nc.vector.tensor_add(out=t_t[:], in0=t_t[:], in1=prm[:, 16:24])
            return s_t, t_t

        def ft_transposes():
            words = ftraw[:].bitcast(F32)
            bank = psum.tile([P, 4, B], F32, tag="bank", name="ftbank")
            for kc in range(4):
                nc.tensor.transpose(bank[:, kc, :], words[:, kc * P : (kc + 1) * P], ident_f[:])
            nc.scalar.copy(out=ftT[:], in_=bank[:].rearrange("p k b -> p (k b)"))

        wfts = {}

        def gate_transposes(ot):
            bank = psum.tile([P, 4, P], F32, tag="bank", name="wfbank")
            words = wfraw[ot // 2][:, ot % 2, :].bitcast(F32)
            for kc in range(4):
                nc.tensor.transpose(bank[:, kc, :], words[:, kc * P : (kc + 1) * P], ident_f[:])
            wft = stage.tile([P, 4 * P], F32, tag="wft", bufs=4, name="wft")
            nc.scalar.copy(out=wft[:], in_=bank[:].rearrange("p k o -> p (k o)"))
            wfts[ot] = wft

        gts = {}

        def gate_tile(ot):
            wv = wfts[ot][:].bitcast(BF16).rearrange("p (k o e) -> p k o e", k=4, o=P, e=2)
            fvw = ftT[:].bitcast(BF16).rearrange("p (k b e) -> p k b e", k=4, b=B, e=2)
            acc = psum.tile([P, P], F32, tag="bank", name="gbank")
            for kc in range(4):
                for e in range(2):
                    nc.tensor.matmul(
                        acc[:],
                        lhsT=wv[:, kc, :, e],
                        rhs=fvw[:, kc, :, e],
                        start=(kc == 0 and e == 0),
                        stop=(kc == 3 and e == 1),
                    )
            if ot % 2 == 0:
                gt = stage.tile([P, 2 * B], F32, tag="gt", bufs=2, align_bytes=64, name="gt%d" % ot)
                gts[ot // 2] = gt
            half = slice(ot % 2 * B, (ot % 2 + 1) * B)
            nc.scalar.activation(
                out=gts[ot // 2][:, half], in_=acc[:], func=ACT.Identity, bias=bp1[:, ot : ot + 1], scale=1.0
            )

        def gate_turn(i):
            pair = (2 * i, 2 * i + 1)
            if not any(ot in ON_TENSOR for ot in pair):
                nc.vector.transpose(out=gate[:, 2 * i * P : 2 * (i + 1) * P], in_=gts[i][:])
                return
            for ot in pair:
                half = slice(ot % 2 * B, (ot % 2 + 1) * B)
                if ot in ON_TENSOR:
                    bank = psum.tile([P, P], F32, tag="bank", name="gtbank")
                    nc.tensor.transpose(bank[:], gts[i][:, half], ident_f[:])
                    nc.scalar.copy(out=gate[:, ot * P : (ot + 1) * P], in_=bank[:])
                else:
                    nc.vector.transpose(out=gate[:, ot * P : (ot + 1) * P], in_=gts[i][:, half])

        CHUNKS = ((0, 512), (512, 512), (1024, 128))
        LAST = ((1024, 128), (0, 512), (512, 256), (768, 256))

        def mx_pass(acc, ot, g, c0, n):
            nc.tensor.matmul_mx(
                out=acc[:],
                lhsT=w1c[:, ot, g * P : (g + 1) * P].bitcast(FP8X4),
                lhsT_scale=w1s[:, ot, g * P : (g + 1) * P],
                rhs=fvc[:, g, c0 : c0 + n].bitcast(FP8X4),
                rhs_scale=fvs[:, g, c0 : c0 + n],
                start=(g == 0),
                stop=(g == GROUPS - 1),
            )

        def bn_relu(y, acc, ot, c0, n, s_t, t_t):
            nc.scalar.activation(
                out=y[:, c0 : c0 + n],
                in_=acc[:],
                func=ACT.Relu,
                bias=t_t[:, ot : ot + 1],
                scale=s_t[:, ot : ot + 1],
            )

        def conv(ot, s_t, t_t, chunks, y):
            for c0, n in chunks:
                acc = psum.tile([P, n], F32, tag="bank", name="acc")
                for g in range(GROUPS):
                    mx_pass(acc, ot, g, c0, n)
                bn_relu(y, acc, ot, c0, n, s_t, t_t)

        def new_y(ot):
            y = pools["back"].tile([P, COLS], F32, tag="y", bufs=3, align_bytes=64, name="y%d" % ot)
            return y

        def w_next(ot):
            if ot + 3 < OT:
                w_split(ot + 3)
            if ot + 2 < OT:
                w_quant(ot + 2)

        planes = {}

        def turn(ot, y, chunks, copy=nc.scalar.copy):
            if ot not in planes:
                pl = pools["back"].tile([P, PIX, P], F32, tag="yt", bufs=2, align_bytes=64, name="planes%d" % ot)
                planes[ot] = pl
            for c0, n in chunks:
                x0, nx = c0 // B, n // B
                z = psum.tile([P, nx, P], F32, tag="bank", name="z")
                for i in range(nx):
                    nc.tensor.transpose(z[:, i, :], y[:, (x0 + i) * B : (x0 + i + 1) * B], ident_f[:])
                copy(out=planes[ot][:, x0 : x0 + nx, :], in_=z[:])

        def finish_turned(ot):
            step = 32 if ot == OT - 1 else 64
            for i0 in range(0, P, step):
                osb = pools["back"].tile([P, step, PIX], F32, tag="osb", bufs=4, name="osb%d" % ot)
                o0 = ot * P + i0
                nc.vector.tensor_tensor(
                    out=osb[:].rearrange("b (n i) x -> b n x i", i=2),
                    in0=planes[ot][:, :, i0 : i0 + step].rearrange("b x (n i) -> b n x i", i=2),
                    in1=gate[:, o0 : o0 + step]
                    .rearrange("b (n i) -> b n i", i=2)
                    .unsqueeze(2)
                    .to_broadcast([P, step // 2, PIX, 2]),
                    op=ALU.mult,
                )
                nc.sync.dma_start(
                    out=out_flat[:, o0 * PIX : (o0 + step) * PIX], in_=osb[:].rearrange("b o x -> b (o x)")
                )

        def finish(ot, y, between=None):
            if ot in ON_TENSOR:
                if between is not None:
                    between()
                finish_turned(ot)
                return
            yt = pools["back"].tile([P, COLS], F32, tag="yt", bufs=2, align_bytes=64, name="yt%d" % ot)
            nc.vector.transpose(out=yt[:, 1024:1152], in_=y[:, 1024:1152])
            nc.vector.transpose(out=yt[:, 0:1024], in_=y[:, 0:1024])
            if between is not None:
                between()
            osb = pools["back"].tile([P, P, PIX], F32, tag="osb", bufs=4, name="osb%d" % ot)
            nc.vector.tensor_tensor(
                out=osb[:].rearrange("p (n i) x -> p n x i", i=2),
                in0=yt[:].rearrange("p (x n i) -> p n x i", x=PIX, i=2),
                in1=gate[:, ot * P : (ot + 1) * P]
                .rearrange("p (n i) -> p n i", i=2)
                .unsqueeze(2)
                .to_broadcast([P, P // 2, PIX, 2]),
                op=ALU.mult,
            )
            for i in range(4):
                f0 = (ot * P + 32 * i) * PIX
                nc.sync.dma_start(
                    out=out_rows[:, :, f0 : f0 + 32 * PIX],
                    in_=osb[32 * i : 32 * i + 32, :, :].rearrange("l (j o) x -> l j (o x)", j=4),
                )

        open_acc = {}

        def early(ot, g):
            for c0 in (0, 512):
                if g == 0:
                    acc = psum.tile([P, 512], F32, tag="bank", name="early")
                    open_acc[(ot, c0)] = acc
                mx_pass(open_acc[(ot, c0)], ot, g, c0, 512)

        pinned = {ENG.PE, ENG.DVE, ENG.Activation}
        with tc.tile_pool(name="front", bufs=2) as front:
            pools["front"] = front
            with tc.manual_schedule(engines=pinned):
                load_fv(0)
                load_fv(1)
                load_w(0)
                load_fv(2)
                fv_regroup(0)
                load_fv(3)
                load_w(1)
                load_small()
                load_wf(0)
                fv_regroup(1)
                fv_transposes(0, 0, PIX)
                w_tile(0)
                fv_quant(0)
                fv_regroup(2)
                load_fv(4)
                load_wf(1)
                fv_transposes(1, 0, PIX)
                w_quant(0)
                load_wf(2)
                fv_quant(1)
                fv_regroup(3)
                load_fv(5)
                fv_transposes(2, 0, 6)
                early(0, 0)
                fv_transposes(2, 6, PIX)
                w_tile(1)
                early(0, 1)
                fv_quant(2)
                w_quant(1)
                fv_regroup(4)
                fv_transposes(3, 0, 6)
                early(0, 2)
                fv_transposes(3, 6, PIX)
                for g in range(3):
                    early(1, g)
                ft_transposes()
                gate_transposes(0)
                gate_transposes(1)
                fv_quant(3)
                fv_regroup(5)
                load_wf(3)
                fv_transposes(4, 0, 6)
                early(0, 3)
                fv_transposes(4, 6, PIX)
                s_t, t_t = params()
                gate_transposes(2)
                gate_transposes(3)
                gate_tile(0)
                early(1, 3)
                gate_tile(1)
                load_w(2)
                load_w(3)
                fv_quant(4)
                w_split(2)
                gate_turn(0)
                fv_transposes(5, 0, 6)
                gate_tile(2)
                fv_transposes(5, 6, PIX)
                gate_transposes(4)
                gate_transposes(5)
                early(0, 4)
                gate_tile(3)
                early(1, 4)
                load_w(4)
                fv_quant(5)
        pools["back"] = ctx.enter_context(tc.tile_pool(name="back", bufs=2))
        ys = {}
        with tc.manual_schedule(engines=pinned):
            gate_transposes(6)
            gate_transposes(7)
            w_tile(2)
            for ot in range(2):
                ys[ot] = new_y(ot)
                early(ot, 5)
                bn_relu(ys[ot], open_acc[(ot, 0)], ot, 0, 512, s_t, t_t)
                bn_relu(ys[ot], open_acc[(ot, 512)], ot, 512, 512, s_t, t_t)
                conv(ot, s_t, t_t, CHUNKS[2:], ys[ot])
            w_split(3)
            gate_turn(1)
            w_quant(2)
            gate_tile(4)
            gate_tile(5)
            gate_tile(6)
            gate_tile(7)
            load_w(5)
            w_tile(3)
            finish(0, ys[0], lambda: w_next(1))
            gate_turn(2)
            gate_turn(3)
            for ot in range(2, OT):
                ys[ot] = new_y(ot)
                if ot == OT - 1:
                    conv(ot, s_t, t_t, LAST, ys[ot])
                    finish(ot - 1, ys[ot - 1])
                    turn(ot, ys[ot], LAST[0:2], nc.vector.tensor_copy)
                    turn(ot, ys[ot], LAST[2:])
                else:
                    conv(ot, s_t, t_t, CHUNKS, ys[ot])
                if ot + 4 < OT:
                    load_w(ot + 4)
                if ot + 2 < OT:
                    w_tile(ot + 2)
                if ot in ON_TENSOR and ot < OT - 1:
                    turn(ot, ys[ot], CHUNKS)
                if ot < OT - 1:
                    finish(ot - 1, ys[ot - 1], lambda: w_next(ot))
            finish(OT - 1, ys[OT - 1])
